import numpy as np
import ml_dtypes


def mxq(x, axis, fmt="e4m3"):
    dtype, down = {"e4m3": (ml_dtypes.float8_e4m3fn, 7), "e5m2": (ml_dtypes.float8_e5m2, 14)}[fmt]
    v = np.moveaxis(np.asarray(x, np.float32).astype(ml_dtypes.bfloat16).astype(np.float64), axis, -1)
    blocks = v.reshape(v.shape[:-1] + (-1, 32))
    amax = np.abs(blocks).max(-1, keepdims=True)
    byte = np.maximum(np.where(amax > 0, np.frexp(amax)[1] - 1 + 127, 0) - down, 1)
    scale = np.exp2(byte - 127.0)
    codes = (blocks / scale).astype(np.float32).astype(dtype).astype(np.float64)
    return np.moveaxis((codes * scale).reshape(v.shape), -1, axis)


WIDE = False


def mx_kscale(k):
    if not WIDE:
        return np.ones(k)
    levels = np.array([10, -10, 5, -5, 0])
    if k % 512:
        return np.exp2(np.random.permutation(np.resize(levels, k // 32))).repeat(32)
    a = np.empty((k // 512, 16))
    for p in range(k // 512):
        a[p, :8] = np.random.permutation(np.resize(levels, 8))
        for g in range(8):
            far = levels[np.abs(levels - a[p, g]) >= 10]
            a[p, g + 8] = far[np.random.randint(len(far))]
    return np.exp2(a.ravel()).repeat(32)


BF16 = ml_dtypes.bfloat16


def bf(x):
    return np.asarray(x, np.float32).astype(BF16)


def f64(x):
    return np.asarray(x).astype(np.float64)


B, T, C = 4, 256, 1024
EPS = 1e-8


def sigmoid(z):
    return 1.0 / (1.0 + np.exp(-z))


def setup_inputs():
    s = mx_kscale(C)
    t = mx_kscale(C)
    g = 1.0 / np.sqrt(C)
    return {
        "x": bf(np.random.standard_normal((B, T, C)) * s),
        "a0": bf(np.random.standard_normal((B, C)) * t),
        "b0": bf(0.5 + np.random.uniform(size=(B, C))),
        "x_prev0": bf(np.random.standard_normal((B, C)) * s),
        "w": bf((0.5 + 2.0 * np.random.uniform(size=C)) / T),
        "u": bf(np.random.standard_normal(C) * 0.5),
        "mu_r": bf(np.random.uniform(size=C)),
        "mu_k": bf(np.random.uniform(size=C)),
        "mu_v": bf(np.random.uniform(size=C)),
        "W_r": bf(np.random.standard_normal((C, C)) * g / s[None, :]),
        "W_k": bf(np.random.standard_normal((C, C)) * g / s[None, :]),
        "W_v": bf(np.random.standard_normal((C, C)) * g / s[None, :] * t[:, None]),
        "W_out": bf(np.random.standard_normal((C, C)) * 2.0 * g / t[None, :]),
    }


def reference(x, a0, b0, x_prev0, w, u, mu_r, mu_k, mu_v, W_r, W_k, W_v, W_out):
    x, a0, b0, x_prev0 = f64(x), f64(a0), f64(b0), f64(x_prev0)
    w, u = f64(w), f64(u)
    mu_r, mu_k, mu_v = f64(mu_r), f64(mu_k), f64(mu_v)
    x_shift = np.concatenate([x_prev0[:, None, :], x[:, :-1, :]], axis=1)
    xr = mu_r * x + (1.0 - mu_r) * x_shift
    xk = mu_k * x + (1.0 - mu_k) * x_shift
    xv = mu_v * x + (1.0 - mu_v) * x_shift
    r = sigmoid(mxq(xr, 2, "e4m3") @ mxq(f64(W_r), 1, "e4m3").T)
    k = mxq(xk, 2, "e4m3") @ mxq(f64(W_k), 1, "e4m3").T
    v = mxq(xv, 2, "e4m3") @ mxq(f64(W_v), 1, "e4m3").T
    ek = np.exp(u + k)
    steps = np.arange(1, T + 1).astype(np.float64)
    decay_pow = np.exp(-w[None, :] * steps[:, None])
    a_t = a0[:, None, :] * decay_pow[None]
    b_t = b0[:, None, :] * decay_pow[None]
    wkv = (a_t + ek * v) / (b_t + ek + EPS)
    h = r * wkv
    return mxq(h, 2, "e4m3") @ mxq(f64(W_out), 1, "e4m3").T

@@ -1,0 +1,461 @@
+import math
+from contextlib import ExitStack
+
+import concourse.mybir as mybir
+from concourse.masks import make_identity
+
+F32 = mybir.dt.float32
+BF16 = mybir.dt.bfloat16
+U32 = mybir.dt.uint32
+U8 = mybir.dt.uint8
+I32 = mybir.dt.int32
+FP8X4 = mybir.dt.float8_e4m3fn_x4
+ALU = mybir.AluOpType
+AF = mybir.ActivationFunctionType
+
+P = 128
+C = 1024
+NTOK = 1024
+T = 256
+HALF = 512
+EPS = 1e-8
+FLOPS = 4 * 2 * NTOK * C * C
+
+SCALAR_REGROUPS = (2, 2, 2, 1)
+
+V_W, V_U, V_MUR, V_MUK, V_MUV, V_A0, V_B0 = 0, 1, 2, 3, 4, 5, 9
+
+
+def tile_rwkv_timemix_pa_kernel(
+    tc, x, a0, b0, x_prev0, w, u, mu_r, mu_k, mu_v, W_r, W_k, W_v, W_out, out
+):
+    nc = tc.nc
+    x_flat = x.flatten_outer_dims()
+    out_flat = out.flatten_outer_dims()
+    weights = (W_r, W_k, W_v, W_out)
+    with ExitStack() as ctx:
+        keep = ctx.enter_context(tc.tile_pool(name="keep", bufs=1))
+        gpool = ctx.enter_context(tc.tile_pool(name="gpool", bufs=2))
+        psum = ctx.enter_context(tc.psum_pool(name="psum", bufs=8))
+
+        def bank_tile(name):
+            return psum.tile([P, HALF], F32, tag="ps", name=name)
+
+        sm = keep.tile([P, 512], BF16)
+        nc.vector.memset(sm[:], 0.0)
+        epsT = keep.tile([P, 1], F32)
+        nc.vector.memset(epsT[:], EPS)
+        identF = keep.tile([P, P], F32)
+        make_identity(nc, identF[:])
+        identB = keep.tile([P, P], BF16)
+        make_identity(nc, identB[:])
+        negB = keep.tile([P, P], BF16)
+        nc.vector.tensor_scalar_mul(out=negB[:], in0=identB[:], scalar1=-1.0)
+        iota_i = keep.tile([P, T], I32)
+        nc.gpsimd.iota(iota_i[:], pattern=[[1, T]], base=1, channel_multiplier=0)
+        iota1 = keep.tile([P, T], F32)
+        nc.vector.tensor_copy(out=iota1[:], in_=iota_i[:])
+        smt = keep.tile([P, 32, 2], F32)
+        sc = keep.tile([P, P], F32)
+        negw = keep.tile([P, 8], F32)
+        rb = keep.tile([P, 32], F32)
+        alpha = keep.tile([P, 32], F32)
+        gbias = keep.tile([P, 32], F32)
+
+        def scal(v, m):
+            return sc[:, 8 * v + m : 8 * v + m + 1]
+
+        wc = [keep.tile([P, 4, 2, T], U32, align_bytes=64, name="wc%d" % i) for i in range(3)]
+        ws = [keep.tile([P, 4, 2, T], U8, align_bytes=64, name="ws%d" % i) for i in range(3)]
+        woc = keep.tile([P, 2, C], U32, align_bytes=64)
+        wos = keep.tile([P, 2, C], U8, align_bytes=64)
+        xc = [keep.tile([P, 2, NTOK], U32, align_bytes=64, name="xc%d" % i) for i in range(3)]
+        xsc = [keep.tile([P, 2, NTOK], U8, align_bytes=64, name="xsc%d" % i) for i in range(3)]
+        hc = keep.tile([P, 2, NTOK], U32, align_bytes=64)
+        hs = keep.tile([P, 2, NTOK], U8, align_bytes=64)
+        q = keep.tile([P, 8, NTOK], F32)
+        gam = {}
+
+        def sigmoid_table(grp, part):
+            h, g = grp // 2, grp % 2
+            if part == 0:
+                gam[grp] = gpool.tile([P, 4, HALF], F32, tag="gam", name="gam")
+            for j in (2 * part, 2 * part + 1):
+                for bb in range(2):
+                    m, b = 4 * g + j, 2 * h + bb
+                    nc.scalar.activation(
+                        out=gam[grp][:, j, T * bb : T * bb + T],
+                        in_=iota1[:],
+                        func=AF.Sigmoid,
+                        scale=negw[:, m : m + 1],
+                        bias=gbias[:, 8 * b + m : 8 * b + m + 1],
+                    )
+
+        wnat, wgt = {}, {}
+
+        def w_load(pool, s):
+            wi, t4 = s // 4, s % 4
+            if wi < 3:
+                view = weights[wi].rearrange("(g r u e) c -> r g u e c", r=P, u=2, e=2)[:, t4 // 2, t4 % 2, :, :]
+            else:
+                view = weights[wi].rearrange("(t e r) c -> r t e c", r=P, e=2)[:, t4, :, :]
+            wn = pool.tile([P, 2, C], BF16, tag="wnat", bufs=3, name="wnat")
+            nc.sync.dma_start(out=wn[:, :, :], in_=view)
+            wnat[s] = wn
+
+        def w_transposes(s, g):
+            bank = bank_tile("ps_w")
+            for uu in range(2):
+                for blk in range(2):
+                    col = (2 * uu + blk) * P
+                    nc.tensor.transpose(
+                        bank[:, col : col + P],
+                        wnat[s][:, blk, :].bitcast(F32)[:, 256 * g + uu : 256 * g + 256 : 2],
+                        identF[:],
+                    )
+            return bank
+
+        def w_evac(pool, s, g, bank):
+            if g == 0:
+                wgt[s] = pool.tile([P, 2, HALF], F32, tag="wg", bufs=2, align_bytes=64, name="wg")
+            nc.scalar.copy(
+                out=wgt[s][:, g, :].rearrange("p (o u) -> p o u", u=2),
+                in_=bank[:].rearrange("p (u o) -> p o u", u=2),
+            )
+
+        def w_quant(s):
+            wi, t4 = s // 4, s % 4
+            if wi == 3:
+                for g in range(2):
+                    nc.vector.quantize_mx(
+                        out=woc[:, g, T * t4 : T * t4 + T].bitcast(FP8X4),
+                        scales=wos[:, g, T * t4 : T * t4 + T],
+                        in_=wgt[s][:, g, :].bitcast(BF16),
+                    )
+            else:
+                nc.vector.quantize_mx(
+                    out=wc[wi][:, t4, :, :].rearrange("p g o -> p (g o)").bitcast(FP8X4),
+                    scales=ws[wi][:, t4, :, :].rearrange("p g o -> p (g o)"),
+                    in_=wgt[s][:].rearrange("p g w -> p (g w)").bitcast(BF16),
+                )
+
+        def mixes_and_weights(pa):
+            xs_nat, x_nat, xsT, dbank, planes = {}, {}, {}, {}, {}
+
+            def load_x(h, pieces):
+                xs_t = pa.tile([P, 4, C], BF16, tag="xnat", bufs=4, name="xs_nat")
+                x_t = pa.tile([P, 4, C], BF16, tag="xnat", bufs=4, name="x_nat")
+                xs_nat[h] = xs_t
+                x_nat[h] = x_t
+                rows = x_flat[HALF * h : HALF * h + HALF, :]
+                by_batch = rows.rearrange("(k p) c -> p k c", p=T)
+                width = C // pieces
+                for n in range(pieces):
+                    cs = slice(width * n, width * n + width)
+                    nc.sync.dma_start(out=xs_t[8:128, 0:4:2, cs], in_=by_batch[7:127, :, cs])
+                    nc.sync.dma_start(out=xs_t[:, 1:4:2, cs], in_=by_batch[127:255, :, cs])
+                    nc.sync.dma_start(out=x_t[:, :, cs], in_=rows[:, cs].rearrange("(i p) c -> p i c", p=P))
+                    if n == 0:
+                        nc.sync.dma_start(out=xs_t[1:8, 0:4:2, :], in_=by_batch[0:7, :, :])
+                        nc.sync.dma_start(
+                            out=xs_t[0:1, 0:4:2, :],
+                            in_=x_prev0[2 * h : 2 * h + 2, :].rearrange("(o b) c -> o b c", o=1),
+                        )
+
+            def shifted_block(h, gu):
+                bank = bank_tile("ps_xs")
+                for i in range(4):
+                    nc.tensor.transpose(
+                        bank[:, P * i : P * i + P],
+                        xs_nat[h][:, i, :].bitcast(F32)[:, 256 * (gu // 2) + gu % 2 : 256 * (gu // 2) + 256 : 2],
+                        identF[:],
+                    )
+                t = pa.tile([P, HALF], F32, tag="xsT", bufs=5, name="xsT")
+                if h == 1:
+                    nc.scalar.copy(out=t[:], in_=bank[:])
+                else:
+                    nc.vector.tensor_copy(out=t[:], in_=bank[:])
+                xsT[(h, gu)] = t
+
+            def difference_plane(s):
+                h, m = s // 8, s % 8
+                bank = bank_tile("ps_d")
+                lo, hi = 512 * (m // 4) + m % 4, 512 * (m // 4) + 512
+                for i in range(4):
+                    nc.tensor.matmul(
+                        bank[:, P * i : P * i + P], lhsT=x_nat[h][:, i, lo:hi:4], rhs=identB[:],
+                        start=True, stop=False,
+                    )
+                    nc.tensor.matmul(
+                        bank[:, P * i : P * i + P], lhsT=xs_nat[h][:, i, lo:hi:4], rhs=negB[:],
+                        start=False, stop=True,
+                    )
+                dbank[s] = bank
+
+            def mix_plane(s):
+                h, m = s // 8, s % 8
+                gu, e, j, grp = m // 2, m % 2, m % 4, s // 4
+                if j == 0:
+                    planes[grp] = [
+                        pa.tile([P, 4, HALF], BF16, tag="planes", bufs=6, name="planes%d" % i) for i in range(3)
+                    ]
+                shifted = xsT[(h, gu)][:].bitcast(BF16).rearrange("p (t e) -> p t e", e=2)[:, :, e]
+                for mix in range(3):
+                    nc.vector.scalar_tensor_tensor(
+                        out=planes[grp][mix][:, j, :],
+                        in0=dbank[s][:],
+                        scalar=scal(V_MUR + mix, m),
+                        in1=shifted,
+                        op0=ALU.mult,
+                        op1=ALU.add,
+                    )
+
+            def regroup(grp, mix):
+                grouped = pa.tile([P, HALF, 4], BF16, tag="grouped", bufs=3, align_bytes=64, name="grouped")
+                dst = grouped[:].rearrange("p (c i) j -> p c j i", i=4)
+                src = planes[grp][mix][:].rearrange("p j (c i) -> p c j i", i=4)
+                if mix < SCALAR_REGROUPS[grp]:
+                    nc.scalar.copy(out=dst, in_=src)
+                else:
+                    nc.vector.tensor_copy(out=dst, in_=src)
+                return (grp, mix, grouped)
+
+            def quantise_mix(item):
+                grp, mix, grouped = item
+                h, g = grp // 2, grp % 2
+                tok = slice(HALF * h, HALF * h + HALF)
+                nc.vector.quantize_mx(
+                    out=xc[mix][:, g, tok].bitcast(FP8X4),
+                    scales=xsc[mix][:, g, tok],
+                    in_=grouped[:].rearrange("p t j -> p (t j)"),
+                )
+
+            def ln_table(n):
+                m, b = n // 4, n % 4
+                nc.scalar.activation(
+                    out=q[:, m, T * b : T * b + T], in_=dec[:, m, :], func=AF.Ln,
+                    scale=scal(V_B0 + b, m), bias=epsT[:],
+                )
+
+            for v, vec in ((V_W, w), (V_U, u), (V_MUR, mu_r), (V_MUK, mu_k), (V_MUV, mu_v)):
+                nc.scalar.dma_start(out=sm[2 * v : 2 * v + 2, :], in_=vec.rearrange("(r c) -> r c", c=512))
+            nc.scalar.dma_start(out=sm[2 * V_A0 : 2 * V_A0 + 8, :], in_=a0.rearrange("b (r c) -> (b r) c", c=512))
+            nc.scalar.dma_start(out=sm[2 * V_B0 : 2 * V_B0 + 8, :], in_=b0.rearrange("b (r c) -> (b r) c", c=512))
+            load_x(0, 2)
+            for s in range(3):
+                w_load(pa, s)
+            load_x(1, 1)
+
+            ps_sm = bank_tile("ps_sm")
+            for uu in range(2):
+                nc.tensor.transpose(ps_sm[:, P * uu : P * uu + P], sm[:].bitcast(F32)[:, uu:256:2], identF[:])
+            nc.vector.tensor_copy(
+                out=smt[:], in_=ps_sm[:, 0:256].rearrange("p (u r) -> p r u", u=2)[:, 0:32, :]
+            )
+            nc.vector.tensor_copy(out=sc[:], in_=smt[:].rearrange("p r u -> p (r u)").bitcast(BF16))
+            nc.vector.tensor_scalar_mul(out=negw[:], in0=sc[:, 8 * V_W : 8 * V_W + 8], scalar1=-1.0)
+            dec = gpool.tile([P, 8, T], F32, tag="gam", name="dec")
+            for m in range(8):
+                nc.scalar.activation(out=dec[:, m, :], in_=iota1[:], func=AF.Exp, scale=negw[:, m : m + 1])
+            nc.scalar.activation(out=gbias[:], in_=sc[:, 8 * V_B0 : 8 * V_B0 + 32], func=AF.Ln)
+            for gu in range(4):
+                shifted_block(0, gu)
+            difference_plane(0)
+            difference_plane(1)
+            nc.vector.reciprocal(out=rb[:], in_=sc[:, 8 * V_B0 : 8 * V_B0 + 32])
+            nc.vector.tensor_tensor(out=alpha[:], in0=sc[:, 8 * V_A0 : 8 * V_A0 + 32], in1=rb[:], op=ALU.mult)
+            nc.vector.tensor_scalar_add(out=gbias[:], in0=gbias[:], scalar1=-math.log(EPS))
+
+            to_quantise = {}
+            for s in range(16):
+                if s + 2 < 16:
+                    difference_plane(s + 2)
+                banks = [w_transposes(s, g) for g in range(2)] if s < 12 else []
+                if s + 3 < 12:
+                    w_load(pa, s + 3)
+                if 3 <= s < 7:
+                    shifted_block(1, s - 3)
+                for g in range(len(banks)):
+                    w_evac(pa, s, g, banks[g])
+                for n in range(3 * s, min(3 * s + 3, 32)):
+                    ln_table(n)
+                if s >= 4 and s % 4 < SCALAR_REGROUPS[s // 4 - 1]:
+                    to_quantise[s + 1] = [regroup(s // 4 - 1, s % 4)]
+                if s >= 12:
+                    sigmoid_table((s - 12) // 2, s % 2)
+                mix_plane(s)
+                if 0 < s < 13:
+                    w_quant(s - 1)
+                for item in to_quantise.get(s, []):
+                    quantise_mix(item)
+                if s % 4 == 3:
+                    to_quantise[s + 1] = [regroup(s // 4, mix) for mix in range(SCALAR_REGROUPS[s // 4], 3)]
+            for item in to_quantise[16] + [regroup(3, mix) for mix in range(SCALAR_REGROUPS[3])]:
+                quantise_mix(item)
+
+        def stages(pb):
+            acc, ygrp, wgrp, rgrp, ots, held = {}, {}, {}, {}, {}, {}
+
+            def flat(t):
+                return t[:].rearrange("p j t -> p (j t)")
+
+            def runs_of_four(t, cols):
+                return t[:, :, cols].rearrange("p j (c i) -> p c j i", i=4)
+
+            def stage1_matmuls(un):
+                h, m = un // 8, un % 8
+                tok = slice(HALF * h, HALF * h + HALF)
+                mc = slice(P * (m % 2), P * (m % 2) + P)
+                for wi in (1, 2, 0):
+                    ps = bank_tile("ps_s1")
+                    for g in range(2):
+                        nc.tensor.matmul_mx(
+                            out=ps[:],
+                            lhsT=wc[wi][:, m // 2, g, mc].bitcast(FP8X4),
+                            lhsT_scale=ws[wi][:, m // 2, g, mc],
+                            rhs=xc[wi][:, g, tok].bitcast(FP8X4),
+                            rhs_scale=xsc[wi][:, g, tok],
+                            start=(g == 0),
+                            stop=(g == 1),
+                        )
+                    acc[(un, wi)] = ps
+
+            def out_of_psum(un):
+                h, m = un // 8, un % 8
+                j, grp = un % 4, un // 4
+                tok = slice(HALF * h, HALF * h + HALF)
+                if j == 0:
+                    ygrp[grp] = pb.tile([P, 4, HALF], F32, tag="grp", bufs=6, name="ygrp")
+                    wgrp[grp] = pb.tile([P, 4, HALF], F32, tag="grp", bufs=6, name="wgrp")
+                    rgrp[grp] = pb.tile([P, 4, HALF], F32, tag="grp", bufs=6, name="rgrp")
+                y_t = ygrp[grp][:, j, :]
+                nc.vector.tensor_tensor(out=y_t, in0=acc[(un, 1)][:], in1=q[:, m, tok], op=ALU.subtract)
+                nc.scalar.activation(out=y_t, in_=y_t, func=AF.Sigmoid, bias=scal(V_U, m))
+                nc.scalar.activation(out=rgrp[grp][:, j, :], in_=acc[(un, 0)][:], func=AF.Sigmoid)
+                for bb in range(2):
+                    b = 2 * h + bb
+                    cols = slice(T * bb, T * bb + T)
+                    nc.vector.scalar_tensor_tensor(
+                        out=wgrp[grp][:, j, cols],
+                        in0=gam[grp][:, j, cols],
+                        scalar=alpha[:, 8 * b + m : 8 * b + m + 1],
+                        in1=acc[(un, 2)][:, cols],
+                        op0=ALU.mult,
+                        op1=ALU.subtract,
+                    )
+
+            def gate(grp, lo, hi):
+                cols = slice(lo, hi)
+                grouped = pb.tile([P, hi - lo, 4], BF16, tag="grouped", bufs=2, align_bytes=64, name="grouped")
+                nc.vector.tensor_tensor(
+                    out=grouped[:].rearrange("p (c i) j -> p c j i", i=4),
+                    in0=runs_of_four(wgrp[grp], cols),
+                    in1=runs_of_four(rgrp[grp], cols),
+                    op=ALU.mult,
+                )
+                return grouped
+
+            def quantise_h(grp, lo, hi, grouped):
+                h, g = grp // 2, grp % 2
+                tok = slice(HALF * h + lo, HALF * h + hi)
+                nc.vector.quantize_mx(
+                    out=hc[:, g, tok].bitcast(FP8X4),
+                    scales=hs[:, g, tok],
+                    in_=grouped[:].rearrange("p t j -> p (t j)"),
+                )
+
+            def group_step(grp, k):
+                h, g = grp // 2, grp % 2
+                if k == 0:
+                    nc.vector.tensor_tensor(out=flat(wgrp[grp]), in0=flat(wgrp[grp]), in1=flat(ygrp[grp]), op=ALU.mult)
+                elif k == 1:
+                    for j in range(4):
+                        for bb in range(2):
+                            m, b = 4 * g + j, 2 * h + bb
+                            cols = slice(T * bb, T * bb + T)
+                            nc.vector.scalar_tensor_tensor(
+                                out=wgrp[grp][:, j, cols],
+                                in0=gam[grp][:, j, cols],
+                                scalar=alpha[:, 8 * b + m : 8 * b + m + 1],
+                                in1=wgrp[grp][:, j, cols],
+                                op0=ALU.mult,
+                                op1=ALU.subtract,
+                            )
+                elif k == 2:
+                    held[grp] = gate(grp, 0, HALF)
+                else:
+                    quantise_h(grp, 0, HALF, held[grp])
+
+            def stage2_pass(h, n, g, ps):
+                tt, oh = n // 2, n % 2
+                t0 = HALF * h + P * tt
+                nc.tensor.matmul_mx(
+                    out=ps[:],
+                    lhsT=hc[:, g, t0 : t0 + P].bitcast(FP8X4),
+                    lhsT_scale=hs[:, g, t0 : t0 + P],
+                    rhs=woc[:, g, HALF * oh : HALF * oh + HALF].bitcast(FP8X4),
+                    rhs_scale=wos[:, g, HALF * oh : HALF * oh + HALF],
+                    start=(g == 0),
+                    stop=(g == 1),
+                )
+
+            def stage2_out(h, n, ps, on_scalar):
+                tt, oh = n // 2, n % 2
+                t0 = HALF * h + P * tt
+                if n % 4 == 0:
+                    ots[h] = pb.tile([P, 2, C], F32, tag="ot", bufs=2, name="ot")
+                dst = ots[h][:, tt % 2, HALF * oh : HALF * oh + HALF]
+                if on_scalar:
+                    nc.scalar.copy(out=dst, in_=ps[:])
+                else:
+                    nc.vector.tensor_copy(out=dst, in_=ps[:])
+                if oh == 1:
+                    nc.sync.dma_start(out=out_flat[t0 : t0 + P, :], in_=ots[h][:, tt % 2, :])
+
+            for s in range(12, 15):
+                w_load(pb, s)
+            for un in range(4):
+                stage1_matmuls(un)
+                out_of_psum(un)
+            open_banks = []
+            for grp in range(4):
+                for k in range(4):
+                    if grp < 3:
+                        stage1_matmuls(4 * grp + 4 + k)
+                        out_of_psum(4 * grp + 4 + k)
+                    if grp < 3 or k < 2:
+                        group_step(grp, k)
+                    if grp == 0:
+                        banks = [w_transposes(12 + k, g) for g in range(2)]
+                        if k == 0:
+                            w_load(pb, 15)
+                        for g in range(2):
+                            w_evac(pb, 12 + k, g, banks[g])
+                        if k > 0:
+                            w_quant(11 + k)
+                    if grp == 1 and k == 0:
+                        w_quant(15)
+                    if grp < 2 and k >= 2:
+                        sigmoid_table(grp + 2, k - 2)
+                    if grp == 2:
+                        for n in (2 * k, 2 * k + 1):
+                            ps = bank_tile("ps_s2")
+                            stage2_pass(0, n, 0, ps)
+                            stage2_pass(0, n, 1, ps)
+                            stage2_out(0, n, ps, True)
+                    if grp == 3 and k == 0:
+                        for n in range(8):
+                            open_banks.append(bank_tile("ps_s2"))
+                            stage2_pass(1, n, 0, open_banks[n])
+            parts = ((0, T), (T, HALF))
+            last = [gate(3, lo, hi) for lo, hi in parts]
+            for (lo, hi), grouped in zip(parts, last):
+                quantise_h(3, lo, hi, grouped)
+            for n in range(8):
+                stage2_pass(1, n, 1, open_banks[n])
+                stage2_out(1, n, open_banks[n], n % 2 == 0)
+
+        with tc.tile_pool(name="pa", bufs=2) as pool_a:
+            mixes_and_weights(pool_a)
+        with tc.tile_pool(name="pb", bufs=2) as pool_b:
+            stages(pool_b)

@@ -8,7 +8,6 @@ F32 = mybir.dt.float32
 BF16 = mybir.dt.bfloat16
 U32 = mybir.dt.uint32
 U8 = mybir.dt.uint8
-I32 = mybir.dt.int32
 FP8X4 = mybir.dt.float8_e4m3fn_x4
 ALU = mybir.AluOpType
 AF = mybir.ActivationFunctionType
@@ -21,9 +20,10 @@ HALF = 512
 EPS = 1e-8
 FLOPS = 4 * 2 * NTOK * C * C
 
-SCALAR_REGROUPS = (2, 2, 2, 1)
+TENSOR_GRP = 1
+VECTOR_UNITS = tuple(un for un in range(16) if un // 4 != TENSOR_GRP)
 
-V_W, V_U, V_MUR, V_MUK, V_MUV, V_A0, V_B0 = 0, 1, 2, 3, 4, 5, 9
+V_W, V_U, V_MUR, V_MUK, V_MUV, V_A0, V_B0, V_XP = 0, 1, 2, 3, 4, 5, 9, 13
 
 
 def tile_rwkv_timemix_pa_kernel(
@@ -35,14 +35,15 @@ def tile_rwkv_timemix_pa_kernel(
     weights = (W_r, W_k, W_v, W_out)
     with ExitStack() as ctx:
         keep = ctx.enter_context(tc.tile_pool(name="keep", bufs=1))
-        gpool = ctx.enter_context(tc.tile_pool(name="gpool", bufs=2))
+        gpool = ctx.enter_context(tc.tile_pool(name="gpool", bufs=3))
         psum = ctx.enter_context(tc.psum_pool(name="psum", bufs=8))
 
         def bank_tile(name):
             return psum.tile([P, HALF], F32, tag="ps", name=name)
 
         sm = keep.tile([P, 512], BF16)
-        nc.vector.memset(sm[:], 0.0)
+        nc.vector.memset(sm[32:64, :], 0.0)
+        nc.vector.memset(sm[64:P, :], 0.0)
         epsT = keep.tile([P, 1], F32)
         nc.vector.memset(epsT[:], EPS)
         identF = keep.tile([P, P], F32)
@@ -51,12 +52,15 @@ def tile_rwkv_timemix_pa_kernel(
         make_identity(nc, identB[:])
         negB = keep.tile([P, P], BF16)
         nc.vector.tensor_scalar_mul(out=negB[:], in0=identB[:], scalar1=-1.0)
-        iota_i = keep.tile([P, T], I32)
-        nc.gpsimd.iota(iota_i[:], pattern=[[1, T]], base=1, channel_multiplier=0)
+        diffB = keep.tile([P, P], BF16)
+        nc.vector.tensor_copy(out=diffB[:, 0:1], in_=identB[:, 0:1])
+        nc.vector.tensor_tensor(out=diffB[:, 1:P], in0=identB[:, 1:P], in1=identB[:, 0 : P - 1], op=ALU.subtract)
         iota1 = keep.tile([P, T], F32)
-        nc.vector.tensor_copy(out=iota1[:], in_=iota_i[:])
-        smt = keep.tile([P, 32, 2], F32)
-        sc = keep.tile([P, P], F32)
+        nc.gpsimd.iota(
+            iota1[:], pattern=[[1, T]], base=1, channel_multiplier=0, allow_small_or_imprecise_dtypes=True
+        )
+        smt = keep.tile([P, 40, 2], F32)
+        sc = keep.tile([P, 160], F32)
         negw = keep.tile([P, 8], F32)
         rb = keep.tile([P, 32], F32)
         alpha = keep.tile([P, 32], F32)
@@ -76,20 +80,27 @@ def tile_rwkv_timemix_pa_kernel(
         q = keep.tile([P, 8, NTOK], F32)
         gam = {}
 
-        def sigmoid_table(grp, part):
+        def sigmoid_table(grp, j):
             h, g = grp // 2, grp % 2
-            if part == 0:
+            if j == 0:
                 gam[grp] = gpool.tile([P, 4, HALF], F32, tag="gam", name="gam")
-            for j in (2 * part, 2 * part + 1):
-                for bb in range(2):
-                    m, b = 4 * g + j, 2 * h + bb
-                    nc.scalar.activation(
-                        out=gam[grp][:, j, T * bb : T * bb + T],
-                        in_=iota1[:],
-                        func=AF.Sigmoid,
-                        scale=negw[:, m : m + 1],
-                        bias=gbias[:, 8 * b + m : 8 * b + m + 1],
-                    )
+            for bb in range(2):
+                m, b = 4 * g + j, 2 * h + bb
+                nc.scalar.activation(
+                    out=gam[grp][:, j, T * bb : T * bb + T],
+                    in_=iota1[:],
+                    func=AF.Sigmoid,
+                    scale=negw[:, m : m + 1],
+                    bias=gbias[:, 8 * b + m : 8 * b + m + 1],
+                )
+            for bb in range(2):
+                m, b = 4 * g + j, 2 * h + bb
+                nc.scalar.activation(
+                    out=gam[grp][:, j, T * bb : T * bb + T],
+                    in_=gam[grp][:, j, T * bb : T * bb + T],
+                    func=AF.Copy,
+                    scale=alpha[:, 8 * b + m : 8 * b + m + 1],
+                )
 
         wnat, wgt = {}, {}
 
@@ -140,42 +151,53 @@ def tile_rwkv_timemix_pa_kernel(
                 )
 
         def mixes_and_weights(pa):
-            xs_nat, x_nat, xsT, dbank, planes = {}, {}, {}, {}, {}
+            x_nat, dbank, planes, t_grouped = {}, {}, {}, {}
+            diag = pa.tile([P, 2, 3, 4, P], BF16, bufs=1, name="diag")
+            xw = pa.tile([P, 4, 4, T + 1], F32, bufs=1, name="xw")
 
             def load_x(h, pieces):
-                xs_t = pa.tile([P, 4, C], BF16, tag="xnat", bufs=4, name="xs_nat")
-                x_t = pa.tile([P, 4, C], BF16, tag="xnat", bufs=4, name="x_nat")
-                xs_nat[h] = xs_t
+                x_t = pa.tile([P, 4, C], BF16, tag="xnat", bufs=2, name="x_nat")
                 x_nat[h] = x_t
                 rows = x_flat[HALF * h : HALF * h + HALF, :]
-                by_batch = rows.rearrange("(k p) c -> p k c", p=T)
                 width = C // pieces
                 for n in range(pieces):
                     cs = slice(width * n, width * n + width)
-                    nc.sync.dma_start(out=xs_t[8:128, 0:4:2, cs], in_=by_batch[7:127, :, cs])
-                    nc.sync.dma_start(out=xs_t[:, 1:4:2, cs], in_=by_batch[127:255, :, cs])
                     nc.sync.dma_start(out=x_t[:, :, cs], in_=rows[:, cs].rearrange("(i p) c -> p i c", p=P))
-                    if n == 0:
-                        nc.sync.dma_start(out=xs_t[1:8, 0:4:2, :], in_=by_batch[0:7, :, :])
-                        nc.sync.dma_start(
-                            out=xs_t[0:1, 0:4:2, :],
-                            in_=x_prev0[2 * h : 2 * h + 2, :].rearrange("(o b) c -> o b c", o=1),
-                        )
 
-            def shifted_block(h, gu):
-                bank = bank_tile("ps_xs")
+            def x_words(h, gu):
+                bank = bank_tile("ps_x")
                 for i in range(4):
                     nc.tensor.transpose(
                         bank[:, P * i : P * i + P],
-                        xs_nat[h][:, i, :].bitcast(F32)[:, 256 * (gu // 2) + gu % 2 : 256 * (gu // 2) + 256 : 2],
+                        x_nat[h][:, i, :].bitcast(F32)[:, 256 * (gu // 2) + gu % 2 : 256 * (gu // 2) + 256 : 2],
                         identF[:],
                     )
-                t = pa.tile([P, HALF], F32, tag="xsT", bufs=5, name="xsT")
+                dst = xw[:, gu, 2 * h : 2 * h + 2, 1 : T + 1]
+                src = bank[:].rearrange("p (b t) -> p b t", t=T)
                 if h == 1:
-                    nc.scalar.copy(out=t[:], in_=bank[:])
+                    nc.scalar.copy(out=dst, in_=src)
                 else:
-                    nc.vector.tensor_copy(out=t[:], in_=bank[:])
-                xsT[(h, gu)] = t
+                    nc.vector.tensor_copy(out=dst, in_=src)
+
+            def t_mix(mix, i):
+                h, g = TENSOR_GRP // 2, TENSOR_GRP % 2
+                bank = bank_tile("ps_t")
+                b, t0 = 2 * h + i // 2, P * (i % 2)
+                for j in range(4):
+                    words = xw[:, 2 * g + j // 2, b, :].bitcast(BF16).rearrange("p (t e) -> p t e", e=2)[:, :, j % 2]
+                    now, before = words[:, t0 + 1 : t0 + 1 + P], words[:, t0 : t0 + P]
+                    dst = bank[:, P * j : P * j + P]
+                    nc.tensor.matmul(dst, lhsT=diag[:, 0, mix, j, :], rhs=now, start=True, stop=False)
+                    nc.tensor.matmul(dst, lhsT=diag[:, 1, mix, j, :], rhs=before, start=False, stop=False)
+                    nc.tensor.matmul(dst, lhsT=identB[:], rhs=before, start=False, stop=True)
+                return bank
+
+            def t_evac(mix, i, bank):
+                if i == 0:
+                    t_grouped[mix] = pa.tile([P, HALF, 4], BF16, tag="grouped", bufs=4, align_bytes=64, name="t_grouped")
+                nc.scalar.copy(
+                    out=t_grouped[mix][:, P * i : P * i + P, :], in_=bank[:].rearrange("p (j t) -> p t j", j=4)
+                )
 
             def difference_plane(s):
                 h, m = s // 8, s % 8
@@ -183,12 +205,17 @@ def tile_rwkv_timemix_pa_kernel(
                 lo, hi = 512 * (m // 4) + m % 4, 512 * (m // 4) + 512
                 for i in range(4):
                     nc.tensor.matmul(
-                        bank[:, P * i : P * i + P], lhsT=x_nat[h][:, i, lo:hi:4], rhs=identB[:],
+                        bank[:, P * i : P * i + P], lhsT=x_nat[h][:, i, lo:hi:4], rhs=diffB[:],
                         start=True, stop=False,
                     )
+                    if i % 2 == 0:
+                        before = sm[:, m % 4 : 512 : 4]
+                        row = 2 * V_XP + 2 * (2 * h + i // 2) + m // 4
+                    else:
+                        before = x_nat[h][:, i - 1, lo:hi:4]
+                        row = P - 1
                     nc.tensor.matmul(
-                        bank[:, P * i : P * i + P], lhsT=xs_nat[h][:, i, lo:hi:4], rhs=negB[:],
-                        start=False, stop=True,
+                        bank[:, P * i : P * i + 1], lhsT=before, rhs=negB[:, row : row + 1], start=False, stop=True
                     )
                 dbank[s] = bank
 
@@ -199,22 +226,31 @@ def tile_rwkv_timemix_pa_kernel(
                     planes[grp] = [
                         pa.tile([P, 4, HALF], BF16, tag="planes", bufs=6, name="planes%d" % i) for i in range(3)
                     ]
-                shifted = xsT[(h, gu)][:].bitcast(BF16).rearrange("p (t e) -> p t e", e=2)[:, :, e]
+                shifted = xw[:, gu, 2 * h : 2 * h + 2, 0:T].bitcast(BF16).rearrange("p b (t e) -> p b t e", e=2)[:, :, :, e]
                 for mix in range(3):
                     nc.vector.scalar_tensor_tensor(
-                        out=planes[grp][mix][:, j, :],
-                        in0=dbank[s][:],
+                        out=planes[grp][mix][:, j, :].rearrange("p (b t) -> p b t", t=T),
+                        in0=dbank[s][:].rearrange("p (b t) -> p b t", t=T),
                         scalar=scal(V_MUR + mix, m),
                         in1=shifted,
                         op0=ALU.mult,
                         op1=ALU.add,
                     )
 
-            def regroup(grp, mix):
-                grouped = pa.tile([P, HALF, 4], BF16, tag="grouped", bufs=3, align_bytes=64, name="grouped")
+            def regroup(grp, mix, engine):
+                grouped = pa.tile([P, HALF, 4], BF16, tag="grouped", bufs=4, align_bytes=64, name="grouped")
                 dst = grouped[:].rearrange("p (c i) j -> p c j i", i=4)
                 src = planes[grp][mix][:].rearrange("p j (c i) -> p c j i", i=4)
-                if mix < SCALAR_REGROUPS[grp]:
+                if engine == 0:
+                    nc.gpsimd.tensor_scalar(
+                        out=grouped[:],
+                        in0=planes[grp][mix][:].rearrange("p j t -> p t j"),
+                        scalar1=1.0,
+                        scalar2=0.0,
+                        op0=ALU.mult,
+                        op1=ALU.add,
+                    )
+                elif engine == 1:
                     nc.scalar.copy(out=dst, in_=src)
                 else:
                     nc.vector.tensor_copy(out=dst, in_=src)
@@ -237,11 +273,12 @@ def tile_rwkv_timemix_pa_kernel(
                     scale=scal(V_B0 + b, m), bias=epsT[:],
                 )
 
-            for v, vec in ((V_W, w), (V_U, u), (V_MUR, mu_r), (V_MUK, mu_k), (V_MUV, mu_v)):
+            for v, vec in ((V_MUR, mu_r), (V_MUK, mu_k), (V_MUV, mu_v), (V_W, w), (V_U, u)):
                 nc.scalar.dma_start(out=sm[2 * v : 2 * v + 2, :], in_=vec.rearrange("(r c) -> r c", c=512))
-            nc.scalar.dma_start(out=sm[2 * V_A0 : 2 * V_A0 + 8, :], in_=a0.rearrange("b (r c) -> (b r) c", c=512))
-            nc.scalar.dma_start(out=sm[2 * V_B0 : 2 * V_B0 + 8, :], in_=b0.rearrange("b (r c) -> (b r) c", c=512))
             load_x(0, 2)
+            nc.sync.dma_start(out=sm[2 * V_B0 : 2 * V_B0 + 8, :], in_=b0.rearrange("b (r c) -> (b r) c", c=512))
+            nc.sync.dma_start(out=sm[2 * V_A0 : 2 * V_A0 + 8, :], in_=a0.rearrange("b (r c) -> (b r) c", c=512))
+            nc.sync.dma_start(out=sm[2 * V_XP : 2 * V_XP + 8, :], in_=x_prev0.rearrange("b (r c) -> (b r) c", c=512))
             for s in range(3):
                 w_load(pa, s)
             load_x(1, 1)
@@ -250,47 +287,63 @@ def tile_rwkv_timemix_pa_kernel(
             for uu in range(2):
                 nc.tensor.transpose(ps_sm[:, P * uu : P * uu + P], sm[:].bitcast(F32)[:, uu:256:2], identF[:])
             nc.vector.tensor_copy(
-                out=smt[:], in_=ps_sm[:, 0:256].rearrange("p (u r) -> p r u", u=2)[:, 0:32, :]
+                out=smt[:], in_=ps_sm[:, 0:256].rearrange("p (u r) -> p r u", u=2)[:, 0:40, :]
             )
             nc.vector.tensor_copy(out=sc[:], in_=smt[:].rearrange("p r u -> p (r u)").bitcast(BF16))
+            nc.vector.tensor_copy(
+                out=xw[:, :, :, 0].rearrange("p (g u) b -> p g u b", u=2),
+                in_=smt[:, 2 * V_XP : 2 * V_XP + 8, :].rearrange("p (b g) u -> p g u b", g=2),
+            )
             nc.vector.tensor_scalar_mul(out=negw[:], in0=sc[:, 8 * V_W : 8 * V_W + 8], scalar1=-1.0)
+            for mix in range(3):
+                for j in range(4):
+                    mu = scal(V_MUR + mix, 4 * (TENSOR_GRP % 2) + j)
+                    for sign, eye in ((0, identB), (1, negB)):
+                        nc.gpsimd.tensor_scalar(
+                            out=diag[:, sign, mix, j, :], in0=eye[:], scalar1=mu, scalar2=0.0, op0=ALU.mult, op1=ALU.add
+                        )
             dec = gpool.tile([P, 8, T], F32, tag="gam", name="dec")
             for m in range(8):
                 nc.scalar.activation(out=dec[:, m, :], in_=iota1[:], func=AF.Exp, scale=negw[:, m : m + 1])
             nc.scalar.activation(out=gbias[:], in_=sc[:, 8 * V_B0 : 8 * V_B0 + 32], func=AF.Ln)
             for gu in range(4):
-                shifted_block(0, gu)
-            difference_plane(0)
-            difference_plane(1)
+                x_words(0, gu)
+            difference_plane(VECTOR_UNITS[0])
+            difference_plane(VECTOR_UNITS[1])
             nc.vector.reciprocal(out=rb[:], in_=sc[:, 8 * V_B0 : 8 * V_B0 + 32])
             nc.vector.tensor_tensor(out=alpha[:], in0=sc[:, 8 * V_A0 : 8 * V_A0 + 32], in1=rb[:], op=ALU.mult)
             nc.vector.tensor_scalar_add(out=gbias[:], in0=gbias[:], scalar1=-math.log(EPS))
 
-            to_quantise = {}
-            for s in range(16):
-                if s + 2 < 16:
-                    difference_plane(s + 2)
-                banks = [w_transposes(s, g) for g in range(2)] if s < 12 else []
-                if s + 3 < 12:
-                    w_load(pa, s + 3)
-                if 3 <= s < 7:
-                    shifted_block(1, s - 3)
-                for g in range(len(banks)):
-                    w_evac(pa, s, g, banks[g])
-                for n in range(3 * s, min(3 * s + 3, 32)):
-                    ln_table(n)
-                if s >= 4 and s % 4 < SCALAR_REGROUPS[s // 4 - 1]:
-                    to_quantise[s + 1] = [regroup(s // 4 - 1, s % 4)]
-                if s >= 12:
-                    sigmoid_table((s - 12) // 2, s % 2)
-                mix_plane(s)
-                if 0 < s < 13:
-                    w_quant(s - 1)
-                for item in to_quantise.get(s, []):
+            to_quantise = {n: [] for n in range(14)}
+            for n in range(12):
+                if n + 2 < 12:
+                    difference_plane(VECTOR_UNITS[n + 2])
+                banks = [w_transposes(n, g) for g in range(2)]
+                if n + 3 < 12:
+                    w_load(pa, n + 3)
+                if n < 4:
+                    x_words(1, n)
+                t_bank = t_mix(n // 4, n % 4)
+                for g in range(2):
+                    w_evac(pa, n, g, banks[g])
+                t_evac(n // 4, n % 4, t_bank)
+                if n < 8:
+                    for row in range(4 * n, 4 * n + 4):
+                        ln_table(row)
+                else:
+                    sigmoid_table(0, n - 8)
+                if n % 4 == 3:
+                    to_quantise[n + 1].append((TENSOR_GRP, n // 4, t_grouped[n // 4]))
+                if n >= 4 and n % 4 < 3:
+                    to_quantise[n + 2].append(regroup(VECTOR_UNITS[n - 4] // 4, n % 4, 0))
+                mix_plane(VECTOR_UNITS[n])
+                if n > 0:
+                    w_quant(n - 1)
+                for item in to_quantise[n]:
                     quantise_mix(item)
-                if s % 4 == 3:
-                    to_quantise[s + 1] = [regroup(s // 4, mix) for mix in range(SCALAR_REGROUPS[s // 4], 3)]
-            for item in to_quantise[16] + [regroup(3, mix) for mix in range(SCALAR_REGROUPS[3])]:
+            w_quant(11)
+            rest = [regroup(VECTOR_UNITS[11] // 4, mix, mix) for mix in range(3)]
+            for item in to_quantise[12] + rest[::-1]:
                 quantise_mix(item)
 
         def stages(pb):
@@ -332,17 +385,9 @@ def tile_rwkv_timemix_pa_kernel(
                 nc.vector.tensor_tensor(out=y_t, in0=acc[(un, 1)][:], in1=q[:, m, tok], op=ALU.subtract)
                 nc.scalar.activation(out=y_t, in_=y_t, func=AF.Sigmoid, bias=scal(V_U, m))
                 nc.scalar.activation(out=rgrp[grp][:, j, :], in_=acc[(un, 0)][:], func=AF.Sigmoid)
-                for bb in range(2):
-                    b = 2 * h + bb
-                    cols = slice(T * bb, T * bb + T)
-                    nc.vector.scalar_tensor_tensor(
-                        out=wgrp[grp][:, j, cols],
-                        in0=gam[grp][:, j, cols],
-                        scalar=alpha[:, 8 * b + m : 8 * b + m + 1],
-                        in1=acc[(un, 2)][:, cols],
-                        op0=ALU.mult,
-                        op1=ALU.subtract,
-                    )
+                nc.vector.tensor_tensor(
+                    out=wgrp[grp][:, j, :], in0=gam[grp][:, j, :], in1=acc[(un, 2)][:], op=ALU.subtract
+                )
 
             def gate(grp, lo, hi):
                 cols = slice(lo, hi)
@@ -369,18 +414,9 @@ def tile_rwkv_timemix_pa_kernel(
                 if k == 0:
                     nc.vector.tensor_tensor(out=flat(wgrp[grp]), in0=flat(wgrp[grp]), in1=flat(ygrp[grp]), op=ALU.mult)
                 elif k == 1:
-                    for j in range(4):
-                        for bb in range(2):
-                            m, b = 4 * g + j, 2 * h + bb
-                            cols = slice(T * bb, T * bb + T)
-                            nc.vector.scalar_tensor_tensor(
-                                out=wgrp[grp][:, j, cols],
-                                in0=gam[grp][:, j, cols],
-                                scalar=alpha[:, 8 * b + m : 8 * b + m + 1],
-                                in1=wgrp[grp][:, j, cols],
-                                op0=ALU.mult,
-                                op1=ALU.subtract,
-                            )
+                    nc.vector.tensor_tensor(
+                        out=flat(wgrp[grp]), in0=flat(gam[grp]), in1=flat(wgrp[grp]), op=ALU.subtract
+                    )
                 elif k == 2:
                     held[grp] = gate(grp, 0, HALF)
                 else:
@@ -417,6 +453,7 @@ def tile_rwkv_timemix_pa_kernel(
             for un in range(4):
                 stage1_matmuls(un)
                 out_of_psum(un)
+                sigmoid_table(1, un)
             open_banks = []
             for grp in range(4):
                 for k in range(4):
@@ -435,8 +472,8 @@ def tile_rwkv_timemix_pa_kernel(
                             w_quant(11 + k)
                     if grp == 1 and k == 0:
                         w_quant(15)
-                    if grp < 2 and k >= 2:
-                        sigmoid_table(grp + 2, k - 2)
+                    if grp < 2:
+                        sigmoid_table(grp + 2, k)
                     if grp == 2:
                         for n in (2 * k, 2 * k + 1):
                             ps = bank_tile("ps_s2")

@@ -334,16 +334,17 @@ def tile_rwkv_timemix_pa_kernel(
                     sigmoid_table(0, n - 8)
                 if n % 4 == 3:
                     to_quantise[n + 1].append((TENSOR_GRP, n // 4, t_grouped[n // 4]))
-                if n >= 4 and n % 4 < 3:
-                    to_quantise[n + 2].append(regroup(VECTOR_UNITS[n - 4] // 4, n % 4, 0))
+                if n >= 4 and n % 4 == 0:
+                    to_quantise[n + 1].append(regroup(VECTOR_UNITS[n - 4] // 4, 0, 1))
                 mix_plane(VECTOR_UNITS[n])
                 if n > 0:
                     w_quant(n - 1)
                 for item in to_quantise[n]:
                     quantise_mix(item)
+                if n % 4 == 3:
+                    to_quantise[n + 1] += [regroup(VECTOR_UNITS[n] // 4, mix, 2) for mix in (1, 2)]
             w_quant(11)
-            rest = [regroup(VECTOR_UNITS[11] // 4, mix, mix) for mix in range(3)]
-            for item in to_quantise[12] + rest[::-1]:
+            for item in to_quantise[12] + [regroup(VECTOR_UNITS[11] // 4, 0, 1)]:
                 quantise_mix(item)
 
         def stages(pb):

@@ -20,7 +20,17 @@ HALF = 512
 EPS = 1e-8
 FLOPS = 4 * 2 * NTOK * C * C
 
-TENSOR_GRP = 1
+TENSOR_GRP = 3
+W_FIRST = 8
+TABLE0 = {9: (0,), 10: (1, 2), 11: (3,)}
+LATE = (2, 2, 3, 3)
+X_VECTOR = ((0, 0), (0, 1))
+S_MULT = (3,)
+X_STEPS = {1: ((0, 2),), 2: ((0, 3),), 3: ((1, 2),), 4: ((1, 3),), 5: ((1, 0),), 6: ((1, 1),)}
+T_STEPS = (0, 0, 0, 0, 0, 2, 2, 2, 2, 2, 1, 1)
+LN_ROWS = (0, 0, 4, 8, 12, 16, 20, 24, 28, 32, 32, 32, 32)
+S_REGROUPS = {4: ((0, 0),), 8: ((1, 0),)}
+V_REGROUPS = {3: ((0, 1),), 4: ((0, 2),), 7: ((1, 1),), 8: ((1, 2),)}
 VECTOR_UNITS = tuple(un for un in range(16) if un // 4 != TENSOR_GRP)
 
 V_W, V_U, V_MUR, V_MUK, V_MUV, V_A0, V_B0, V_XP = 0, 1, 2, 3, 4, 5, 9, 13
@@ -36,14 +46,13 @@ def tile_rwkv_timemix_pa_kernel(
     with ExitStack() as ctx:
         keep = ctx.enter_context(tc.tile_pool(name="keep", bufs=1))
         gpool = ctx.enter_context(tc.tile_pool(name="gpool", bufs=3))
+        wpool = ctx.enter_context(tc.tile_pool(name="wpool", bufs=2))
+        mid = ctx.enter_context(tc.tile_pool(name="mid", bufs=4))
         psum = ctx.enter_context(tc.psum_pool(name="psum", bufs=8))
 
         def bank_tile(name):
             return psum.tile([P, HALF], F32, tag="ps", name=name)
 
-        sm = keep.tile([P, 512], BF16)
-        nc.vector.memset(sm[32:64, :], 0.0)
-        nc.vector.memset(sm[64:P, :], 0.0)
         epsT = keep.tile([P, 1], F32)
         nc.vector.memset(epsT[:], EPS)
         identF = keep.tile([P, P], F32)
@@ -52,14 +61,10 @@ def tile_rwkv_timemix_pa_kernel(
         make_identity(nc, identB[:])
         negB = keep.tile([P, P], BF16)
         nc.vector.tensor_scalar_mul(out=negB[:], in0=identB[:], scalar1=-1.0)
-        diffB = keep.tile([P, P], BF16)
-        nc.vector.tensor_copy(out=diffB[:, 0:1], in_=identB[:, 0:1])
-        nc.vector.tensor_tensor(out=diffB[:, 1:P], in0=identB[:, 1:P], in1=identB[:, 0 : P - 1], op=ALU.subtract)
         iota1 = keep.tile([P, T], F32)
         nc.gpsimd.iota(
             iota1[:], pattern=[[1, T]], base=1, channel_multiplier=0, allow_small_or_imprecise_dtypes=True
         )
-        smt = keep.tile([P, 40, 2], F32)
         sc = keep.tile([P, 160], F32)
         negw = keep.tile([P, 8], F32)
         rb = keep.tile([P, 32], F32)
@@ -93,7 +98,7 @@ def tile_rwkv_timemix_pa_kernel(
                     scale=negw[:, m : m + 1],
                     bias=gbias[:, 8 * b + m : 8 * b + m + 1],
                 )
-            for bb in range(2):
+            for bb in range(2 if grp in S_MULT else 0):
                 m, b = 4 * g + j, 2 * h + bb
                 nc.scalar.activation(
                     out=gam[grp][:, j, T * bb : T * bb + T],
@@ -104,13 +109,16 @@ def tile_rwkv_timemix_pa_kernel(
 
         wnat, wgt = {}, {}
 
-        def w_load(pool, s):
-            wi, t4 = s // 4, s % 4
+        def weight_tile(s):
+            return ((1, 2, 0)[s % 3], s // 3) if s < 12 else (3, s - 12)
+
+        def w_load(s):
+            wi, t4 = weight_tile(s)
             if wi < 3:
                 view = weights[wi].rearrange("(g r u e) c -> r g u e c", r=P, u=2, e=2)[:, t4 // 2, t4 % 2, :, :]
             else:
                 view = weights[wi].rearrange("(t e r) c -> r t e c", r=P, e=2)[:, t4, :, :]
-            wn = pool.tile([P, 2, C], BF16, tag="wnat", bufs=3, name="wnat")
+            wn = wpool.tile([P, 2, C], BF16, tag="wnat", bufs=3, name="wnat")
             nc.sync.dma_start(out=wn[:, :, :], in_=view)
             wnat[s] = wn
 
@@ -126,16 +134,16 @@ def tile_rwkv_timemix_pa_kernel(
                     )
             return bank
 
-        def w_evac(pool, s, g, bank):
+        def w_evac(s, g, bank):
             if g == 0:
-                wgt[s] = pool.tile([P, 2, HALF], F32, tag="wg", bufs=2, align_bytes=64, name="wg")
+                wgt[s] = wpool.tile([P, 2, HALF], F32, tag="wg", bufs=2, align_bytes=64, name="wg")
             nc.scalar.copy(
                 out=wgt[s][:, g, :].rearrange("p (o u) -> p o u", u=2),
                 in_=bank[:].rearrange("p (u o) -> p o u", u=2),
             )
 
         def w_quant(s):
-            wi, t4 = s // 4, s % 4
+            wi, t4 = weight_tile(s)
             if wi == 3:
                 for g in range(2):
                     nc.vector.quantize_mx(
@@ -150,8 +158,46 @@ def tile_rwkv_timemix_pa_kernel(
                     in_=wgt[s][:].rearrange("p g w -> p (g w)").bitcast(BF16),
                 )
 
+        planes = {}
+
+        def regroup(grp, mix, engine):
+            grouped = mid.tile([P, HALF, 4], BF16, tag="grouped", bufs=4, align_bytes=64, name="grouped")
+            dst = grouped[:].rearrange("p (c i) j -> p c j i", i=4)
+            src = planes[grp][mix][:].rearrange("p j (c i) -> p c j i", i=4)
+            if engine == 0:
+                nc.gpsimd.tensor_scalar(
+                    out=grouped[:],
+                    in0=planes[grp][mix][:].rearrange("p j t -> p t j"),
+                    scalar1=1.0,
+                    scalar2=0.0,
+                    op0=ALU.mult,
+                    op1=ALU.add,
+                )
+            elif engine == 1:
+                nc.scalar.copy(out=dst, in_=src)
+            else:
+                nc.vector.tensor_copy(out=dst, in_=src)
+            return (grp, mix, grouped)
+
+        def quantise_mix(item):
+            grp, mix, grouped = item
+            h, g = grp // 2, grp % 2
+            tok = slice(HALF * h, HALF * h + HALF)
+            nc.vector.quantize_mx(
+                out=xc[mix][:, g, tok].bitcast(FP8X4),
+                scales=xsc[mix][:, g, tok],
+                in_=grouped[:].rearrange("p t j -> p (t j)"),
+            )
+
         def mixes_and_weights(pa):
-            x_nat, dbank, planes, t_grouped = {}, {}, {}, {}
+            sm = pa.tile([P, 512], BF16, bufs=1, name="sm")
+            nc.vector.memset(sm[32:64, :], 0.0)
+            nc.vector.memset(sm[64:P, :], 0.0)
+            diffB = pa.tile([P, P], BF16, bufs=1, name="diffB")
+            nc.vector.tensor_copy(out=diffB[:, 0:1], in_=identB[:, 0:1])
+            nc.vector.tensor_tensor(out=diffB[:, 1:P], in0=identB[:, 1:P], in1=identB[:, 0 : P - 1], op=ALU.subtract)
+            smt = pa.tile([P, 40, 2], F32, bufs=1, name="smt")
+            x_nat, dbank, t_grouped = {}, {}, {}
             diag = pa.tile([P, 2, 3, 4, P], BF16, bufs=1, name="diag")
             xw = pa.tile([P, 4, 4, T + 1], F32, bufs=1, name="xw")
 
@@ -174,10 +220,10 @@ def tile_rwkv_timemix_pa_kernel(
                     )
                 dst = xw[:, gu, 2 * h : 2 * h + 2, 1 : T + 1]
                 src = bank[:].rearrange("p (b t) -> p b t", t=T)
-                if h == 1:
-                    nc.scalar.copy(out=dst, in_=src)
-                else:
+                if (h, gu) in X_VECTOR:
                     nc.vector.tensor_copy(out=dst, in_=src)
+                else:
+                    nc.scalar.copy(out=dst, in_=src)
 
             def t_mix(mix, i):
                 h, g = TENSOR_GRP // 2, TENSOR_GRP % 2
@@ -194,7 +240,7 @@ def tile_rwkv_timemix_pa_kernel(
 
             def t_evac(mix, i, bank):
                 if i == 0:
-                    t_grouped[mix] = pa.tile([P, HALF, 4], BF16, tag="grouped", bufs=4, align_bytes=64, name="t_grouped")
+                    t_grouped[mix] = mid.tile([P, HALF, 4], BF16, tag="grouped", bufs=4, align_bytes=64, name="t_grouped")
                 nc.scalar.copy(
                     out=t_grouped[mix][:, P * i : P * i + P, :], in_=bank[:].rearrange("p (j t) -> p t j", j=4)
                 )
@@ -224,7 +270,7 @@ def tile_rwkv_timemix_pa_kernel(
                 gu, e, j, grp = m // 2, m % 2, m % 4, s // 4
                 if j == 0:
                     planes[grp] = [
-                        pa.tile([P, 4, HALF], BF16, tag="planes", bufs=6, name="planes%d" % i) for i in range(3)
+                        mid.tile([P, 4, HALF], BF16, tag="planes", bufs=6, name="planes%d" % i) for i in range(3)
                     ]
                 shifted = xw[:, gu, 2 * h : 2 * h + 2, 0:T].bitcast(BF16).rearrange("p b (t e) -> p b t e", e=2)[:, :, :, e]
                 for mix in range(3):
@@ -236,35 +282,6 @@ def tile_rwkv_timemix_pa_kernel(
                         op0=ALU.mult,
                         op1=ALU.add,
                     )
-
-            def regroup(grp, mix, engine):
-                grouped = pa.tile([P, HALF, 4], BF16, tag="grouped", bufs=4, align_bytes=64, name="grouped")
-                dst = grouped[:].rearrange("p (c i) j -> p c j i", i=4)
-                src = planes[grp][mix][:].rearrange("p j (c i) -> p c j i", i=4)
-                if engine == 0:
-                    nc.gpsimd.tensor_scalar(
-                        out=grouped[:],
-                        in0=planes[grp][mix][:].rearrange("p j t -> p t j"),
-                        scalar1=1.0,
-                        scalar2=0.0,
-                        op0=ALU.mult,
-                        op1=ALU.add,
-                    )
-                elif engine == 1:
-                    nc.scalar.copy(out=dst, in_=src)
-                else:
-                    nc.vector.tensor_copy(out=dst, in_=src)
-                return (grp, mix, grouped)
-
-            def quantise_mix(item):
-                grp, mix, grouped = item
-                h, g = grp // 2, grp % 2
-                tok = slice(HALF * h, HALF * h + HALF)
-                nc.vector.quantize_mx(
-                    out=xc[mix][:, g, tok].bitcast(FP8X4),
-                    scales=xsc[mix][:, g, tok],
-                    in_=grouped[:].rearrange("p t j -> p (t j)"),
-                )
 
             def ln_table(n):
                 m, b = n // 4, n % 4
@@ -280,9 +297,11 @@ def tile_rwkv_timemix_pa_kernel(
             nc.sync.dma_start(out=sm[2 * V_A0 : 2 * V_A0 + 8, :], in_=a0.rearrange("b (r c) -> (b r) c", c=512))
             nc.sync.dma_start(out=sm[2 * V_XP : 2 * V_XP + 8, :], in_=x_prev0.rearrange("b (r c) -> (b r) c", c=512))
             for s in range(3):
-                w_load(pa, s)
+                w_load(s)
             load_x(1, 1)
 
+            x_words(0, 0)
+            x_words(0, 1)
             ps_sm = bank_tile("ps_sm")
             for uu in range(2):
                 nc.tensor.transpose(ps_sm[:, P * uu : P * uu + P], sm[:].bitcast(F32)[:, uu:256:2], identF[:])
@@ -295,6 +314,8 @@ def tile_rwkv_timemix_pa_kernel(
                 in_=smt[:, 2 * V_XP : 2 * V_XP + 8, :].rearrange("p (b g) u -> p g u b", g=2),
             )
             nc.vector.tensor_scalar_mul(out=negw[:], in0=sc[:, 8 * V_W : 8 * V_W + 8], scalar1=-1.0)
+            difference_plane(VECTOR_UNITS[0])
+            difference_plane(VECTOR_UNITS[1])
             for mix in range(3):
                 for j in range(4):
                     mu = scal(V_MUR + mix, 4 * (TENSOR_GRP % 2) + j)
@@ -302,52 +323,52 @@ def tile_rwkv_timemix_pa_kernel(
                         nc.gpsimd.tensor_scalar(
                             out=diag[:, sign, mix, j, :], in0=eye[:], scalar1=mu, scalar2=0.0, op0=ALU.mult, op1=ALU.add
                         )
+            nc.vector.reciprocal(out=rb[:], in_=sc[:, 8 * V_B0 : 8 * V_B0 + 32])
+            nc.vector.tensor_tensor(out=alpha[:], in0=sc[:, 8 * V_A0 : 8 * V_A0 + 32], in1=rb[:], op=ALU.mult)
+
             dec = gpool.tile([P, 8, T], F32, tag="gam", name="dec")
             for m in range(8):
                 nc.scalar.activation(out=dec[:, m, :], in_=iota1[:], func=AF.Exp, scale=negw[:, m : m + 1])
-            nc.scalar.activation(out=gbias[:], in_=sc[:, 8 * V_B0 : 8 * V_B0 + 32], func=AF.Ln)
-            for gu in range(4):
-                x_words(0, gu)
-            difference_plane(VECTOR_UNITS[0])
-            difference_plane(VECTOR_UNITS[1])
-            nc.vector.reciprocal(out=rb[:], in_=sc[:, 8 * V_B0 : 8 * V_B0 + 32])
-            nc.vector.tensor_tensor(out=alpha[:], in0=sc[:, 8 * V_A0 : 8 * V_A0 + 32], in1=rb[:], op=ALU.mult)
-            nc.vector.tensor_scalar_add(out=gbias[:], in0=gbias[:], scalar1=-math.log(EPS))
-
             to_quantise = {n: [] for n in range(14)}
+            t_next = 0
             for n in range(12):
                 if n + 2 < 12:
                     difference_plane(VECTOR_UNITS[n + 2])
-                banks = [w_transposes(n, g) for g in range(2)]
-                if n + 3 < 12:
-                    w_load(pa, n + 3)
-                if n < 4:
-                    x_words(1, n)
-                t_bank = t_mix(n // 4, n % 4)
-                for g in range(2):
-                    w_evac(pa, n, g, banks[g])
-                t_evac(n // 4, n % 4, t_bank)
-                if n < 8:
-                    for row in range(4 * n, 4 * n + 4):
-                        ln_table(row)
-                else:
-                    sigmoid_table(0, n - 8)
-                if n % 4 == 3:
-                    to_quantise[n + 1].append((TENSOR_GRP, n // 4, t_grouped[n // 4]))
-                if n >= 4 and n % 4 == 0:
-                    to_quantise[n + 1].append(regroup(VECTOR_UNITS[n - 4] // 4, 0, 1))
+                for h, gu in X_STEPS.get(n, ()):
+                    x_words(h, gu)
+                banks = [w_transposes(n, g) for g in range(2)] if n < W_FIRST else []
+                if banks:
+                    w_load(n + 3)
+                if n == 6:
+                    nc.vector.tensor_scalar_add(out=gbias[:], in0=gbias[:], scalar1=-math.log(EPS))
+                t_banks = []
+                for i in range(T_STEPS[n]):
+                    t_banks.append((t_next, t_mix(t_next // 4, t_next % 4)))
+                    t_next += 1
+                for g in range(len(banks)):
+                    w_evac(n, g, banks[g])
+                for t, bank in t_banks:
+                    t_evac(t // 4, t % 4, bank)
+                    if t % 4 == 3:
+                        to_quantise[n + 1].append((TENSOR_GRP, t // 4, t_grouped[t // 4]))
+                if n == 1:
+                    nc.scalar.activation(out=gbias[:], in_=sc[:, 8 * V_B0 : 8 * V_B0 + 32], func=AF.Ln)
+                for row in range(LN_ROWS[n], LN_ROWS[n + 1]):
+                    ln_table(row)
+                for grp, mix in S_REGROUPS.get(n, ()):
+                    to_quantise[n + 2].append(regroup(grp, mix, 1))
+                for j in TABLE0.get(n, ()):
+                    sigmoid_table(0, j)
                 mix_plane(VECTOR_UNITS[n])
-                if n > 0:
+                if 0 < n <= W_FIRST:
                     w_quant(n - 1)
                 for item in to_quantise[n]:
                     quantise_mix(item)
-                if n % 4 == 3:
-                    to_quantise[n + 1] += [regroup(VECTOR_UNITS[n] // 4, mix, 2) for mix in (1, 2)]
-            w_quant(11)
-            for item in to_quantise[12] + [regroup(VECTOR_UNITS[11] // 4, 0, 1)]:
-                quantise_mix(item)
+                for grp, mix in V_REGROUPS.get(n, ()):
+                    to_quantise[n + 1].append(regroup(grp, mix, 2))
+            return [lambda item=item: quantise_mix(item) for item in to_quantise[12] + to_quantise[13]]
 
-        def stages(pb):
+        def stages(pb, late):
             acc, ygrp, wgrp, rgrp, ots, held = {}, {}, {}, {}, {}, {}
 
             def flat(t):
@@ -374,25 +395,45 @@ def tile_rwkv_timemix_pa_kernel(
                         )
                     acc[(un, wi)] = ps
 
-            def out_of_psum(un):
+            def a_minus(grp, j, bb, operand):
+                h, g = grp // 2, grp % 2
+                cols = slice(T * bb, T * bb + T)
+                m, b = 4 * g + j, 2 * h + bb
+                nc.vector.scalar_tensor_tensor(
+                    out=wgrp[grp][:, j, cols],
+                    in0=gam[grp][:, j, cols],
+                    scalar=alpha[:, 8 * b + m : 8 * b + m + 1],
+                    in1=operand,
+                    op0=ALU.mult,
+                    op1=ALU.subtract,
+                )
+
+            def sigmoids(un):
                 h, m = un // 8, un % 8
                 j, grp = un % 4, un // 4
                 tok = slice(HALF * h, HALF * h + HALF)
                 if j == 0:
-                    ygrp[grp] = pb.tile([P, 4, HALF], F32, tag="grp", bufs=6, name="ygrp")
-                    wgrp[grp] = pb.tile([P, 4, HALF], F32, tag="grp", bufs=6, name="wgrp")
-                    rgrp[grp] = pb.tile([P, 4, HALF], F32, tag="grp", bufs=6, name="rgrp")
+                    ygrp[grp] = pb.tile([P, 4, HALF], F32, tag="grp", bufs=5, name="ygrp")
+                    wgrp[grp] = pb.tile([P, 4, HALF], F32, tag="grp", bufs=5, name="wgrp")
+                    rgrp[grp] = pb.tile([P, 4, HALF], F32, tag="grp", bufs=5, name="rgrp")
                 y_t = ygrp[grp][:, j, :]
                 nc.vector.tensor_tensor(out=y_t, in0=acc[(un, 1)][:], in1=q[:, m, tok], op=ALU.subtract)
                 nc.scalar.activation(out=y_t, in_=y_t, func=AF.Sigmoid, bias=scal(V_U, m))
                 nc.scalar.activation(out=rgrp[grp][:, j, :], in_=acc[(un, 0)][:], func=AF.Sigmoid)
-                nc.vector.tensor_tensor(
-                    out=wgrp[grp][:, j, :], in0=gam[grp][:, j, :], in1=acc[(un, 2)][:], op=ALU.subtract
-                )
+
+            def subtract_v(un):
+                j, grp = un % 4, un // 4
+                if grp in S_MULT:
+                    nc.vector.tensor_tensor(
+                        out=wgrp[grp][:, j, :], in0=gam[grp][:, j, :], in1=acc[(un, 2)][:], op=ALU.subtract
+                    )
+                else:
+                    for bb in range(2):
+                        a_minus(grp, j, bb, acc[(un, 2)][:, T * bb : T * bb + T])
 
             def gate(grp, lo, hi):
                 cols = slice(lo, hi)
-                grouped = pb.tile([P, hi - lo, 4], BF16, tag="grouped", bufs=2, align_bytes=64, name="grouped")
+                grouped = mid.tile([P, hi - lo, 4], BF16, tag="grouped", bufs=4, align_bytes=64, name="grouped")
                 nc.vector.tensor_tensor(
                     out=grouped[:].rearrange("p (c i) j -> p c j i", i=4),
                     in0=runs_of_four(wgrp[grp], cols),
@@ -415,9 +456,14 @@ def tile_rwkv_timemix_pa_kernel(
                 if k == 0:
                     nc.vector.tensor_tensor(out=flat(wgrp[grp]), in0=flat(wgrp[grp]), in1=flat(ygrp[grp]), op=ALU.mult)
                 elif k == 1:
-                    nc.vector.tensor_tensor(
-                        out=flat(wgrp[grp]), in0=flat(gam[grp]), in1=flat(wgrp[grp]), op=ALU.subtract
-                    )
+                    if grp in S_MULT:
+                        nc.vector.tensor_tensor(
+                            out=flat(wgrp[grp]), in0=flat(gam[grp]), in1=flat(wgrp[grp]), op=ALU.subtract
+                        )
+                    else:
+                        for j in range(4):
+                            for bb in range(2):
+                                a_minus(grp, j, bb, wgrp[grp][:, j, T * bb : T * bb + T])
                 elif k == 2:
                     held[grp] = gate(grp, 0, HALF)
                 else:
@@ -439,38 +485,60 @@ def tile_rwkv_timemix_pa_kernel(
             def stage2_out(h, n, ps, on_scalar):
                 tt, oh = n // 2, n % 2
                 t0 = HALF * h + P * tt
-                if n % 4 == 0:
-                    ots[h] = pb.tile([P, 2, C], F32, tag="ot", bufs=2, name="ot")
-                dst = ots[h][:, tt % 2, HALF * oh : HALF * oh + HALF]
+                if oh == 0:
+                    ots[h] = mid.tile([P, C], F32, tag="planes", bufs=6, name="ot")
+                dst = ots[h][:, HALF * oh : HALF * oh + HALF]
                 if on_scalar:
                     nc.scalar.copy(out=dst, in_=ps[:])
                 else:
                     nc.vector.tensor_copy(out=dst, in_=ps[:])
                 if oh == 1:
-                    nc.sync.dma_start(out=out_flat[t0 : t0 + P, :], in_=ots[h][:, tt % 2, :])
+                    nc.sync.dma_start(out=out_flat[t0 : t0 + P, :], in_=ots[h][:])
 
-            for s in range(12, 15):
-                w_load(pb, s)
+            w_next = W_FIRST
+            last_regroup = {}
+            def do_regroup(mix):
+                last_regroup[mix] = regroup(2, mix, 2)
+            late = late + [lambda: do_regroup(0), lambda: do_regroup(1), lambda: quantise_mix(last_regroup[0]), lambda: do_regroup(2), lambda: quantise_mix(last_regroup[1]), lambda: quantise_mix(last_regroup[2])]
             for un in range(4):
                 stage1_matmuls(un)
-                out_of_psum(un)
+                if w_next < 12:
+                    banks = [w_transposes(w_next, g) for g in range(2)]
+                    if w_next + 3 < 16:
+                        w_load(w_next + 3)
+                else:
+                    banks = []
+                sigmoids(un)
+                subtract_v(un)
+                for g in range(len(banks)):
+                    w_evac(w_next, g, banks[g])
+                if w_next > W_FIRST:
+                    w_quant(w_next - 1)
+                if banks:
+                    w_next += 1
+                for i in range(LATE[un]):
+                    if late:
+                        late.pop(0)()
                 sigmoid_table(1, un)
             open_banks = []
             for grp in range(4):
                 for k in range(4):
                     if grp < 3:
-                        stage1_matmuls(4 * grp + 4 + k)
-                        out_of_psum(4 * grp + 4 + k)
-                    if grp < 3 or k < 2:
+                        un = 4 * grp + 4 + k
+                        stage1_matmuls(un)
+                        sigmoids(un)
+                        if k > 0:
+                            subtract_v(un)
                         group_step(grp, k)
+                        if k == 0:
+                            subtract_v(un)
                     if grp == 0:
                         banks = [w_transposes(12 + k, g) for g in range(2)]
                         if k == 0:
-                            w_load(pb, 15)
+                            w_load(15)
                         for g in range(2):
-                            w_evac(pb, 12 + k, g, banks[g])
-                        if k > 0:
-                            w_quant(11 + k)
+                            w_evac(12 + k, g, banks[g])
+                        w_quant(11 + k)
                     if grp == 1 and k == 0:
                         w_quant(15)
                     if grp < 2:
@@ -485,15 +553,35 @@ def tile_rwkv_timemix_pa_kernel(
                         for n in range(8):
                             open_banks.append(bank_tile("ps_s2"))
                             stage2_pass(1, n, 0, open_banks[n])
-            parts = ((0, T), (T, HALF))
-            last = [gate(3, lo, hi) for lo, hi in parts]
-            for (lo, hi), grouped in zip(parts, last):
-                quantise_h(3, lo, hi, grouped)
-            for n in range(8):
-                stage2_pass(1, n, 1, open_banks[n])
-                stage2_out(1, n, open_banks[n], n % 2 == 0)
+            def multiply_part(lo, hi):
+                part = wgrp[3][:, :, lo:hi]
+                nc.vector.tensor_tensor(out=part, in0=part, in1=ygrp[3][:, :, lo:hi], op=ALU.mult)
 
-        with tc.tile_pool(name="pa", bufs=2) as pool_a:
-            mixes_and_weights(pool_a)
-        with tc.tile_pool(name="pb", bufs=2) as pool_b:
-            stages(pool_b)
+            def subtract_part(lo, hi):
+                part = wgrp[3][:, :, lo:hi]
+                nc.vector.tensor_tensor(out=part, in0=gam[3][:, :, lo:hi], in1=part, op=ALU.subtract)
+
+            def finish(tiles, on_vector):
+                for n in tiles:
+                    stage2_pass(1, n, 1, open_banks[n])
+                    stage2_out(1, n, open_banks[n], n not in on_vector)
+
+            half_t, last_t = T, T + P
+            multiply_part(0, half_t)
+            subtract_part(0, half_t)
+            multiply_part(half_t, HALF)
+            first = gate(3, 0, half_t)
+            subtract_part(half_t, HALF)
+            quantise_h(3, 0, half_t, first)
+            finish((0, 1, 2, 3), ())
+            second = gate(3, half_t, last_t)
+            third = gate(3, last_t, HALF)
+            quantise_h(3, half_t, last_t, second)
+            quantise_h(3, last_t, HALF, third)
+            finish((4, 5, 6, 7), (5, 7))
+
+        with tc.manual_schedule():
+            with tc.tile_pool(name="pa", bufs=2) as pool_a:
+                late = mixes_and_weights(pool_a)
+            with tc.tile_pool(name="pb", bufs=2) as pool_b:
+                stages(pool_b, late)

@@ -22,15 +22,21 @@ FLOPS = 4 * 2 * NTOK * C * C
 
 TENSOR_GRP = 3
 W_FIRST = 8
+S2_EARLY = 4
+WARM0 = 0
+WARM = (0, 0, 0, 0, 0, 0, 0, 0, 0, 0, 0, 0)
+W_LAG = 1
+W_STEPS = (0, 0, 0, 1, 1, 1, 1, 1, 1, 1, 1, 0)
+S_LATE = (0, 2)
 TABLE0 = {9: (0,), 10: (1, 2), 11: (3,)}
 LATE = (2, 2, 3, 3)
-X_VECTOR = ((0, 0), (0, 1))
+X_VECTOR = ((0, 0),)
 S_MULT = (3,)
 X_STEPS = {1: ((0, 2),), 2: ((0, 3),), 3: ((1, 2),), 4: ((1, 3),), 5: ((1, 0),), 6: ((1, 1),)}
-T_STEPS = (0, 0, 0, 0, 0, 2, 2, 2, 2, 2, 1, 1)
-LN_ROWS = (0, 0, 4, 8, 12, 16, 20, 24, 28, 32, 32, 32, 32)
-S_REGROUPS = {4: ((0, 0),), 8: ((1, 0),)}
-V_REGROUPS = {3: ((0, 1),), 4: ((0, 2),), 7: ((1, 1),), 8: ((1, 2),)}
+T_STEPS = (0, 0, 0, 0, 0, 1, 1, 2, 2, 2, 2, 2)
+LN_ROWS = (0, 4, 8, 12, 16, 20, 24, 28, 32, 32, 32, 32, 32)
+S_REGROUPS = {}
+V_REGROUPS = {3: ((0, 0), (0, 1), (0, 2)), 7: ((1, 0), (1, 1), (1, 2))}
 VECTOR_UNITS = tuple(un for un in range(16) if un // 4 != TENSOR_GRP)
 
 V_W, V_U, V_MUR, V_MUK, V_MUV, V_A0, V_B0, V_XP = 0, 1, 2, 3, 4, 5, 9, 13
@@ -210,6 +216,10 @@ def tile_rwkv_timemix_pa_kernel(
                     cs = slice(width * n, width * n + width)
                     nc.sync.dma_start(out=x_t[:, :, cs], in_=rows[:, cs].rearrange("(i p) c -> p i c", p=P))
 
+            def keep_warm():
+                bank = bank_tile("ps_warm")
+                nc.tensor.matmul(bank[:, 0:P], lhsT=identF[:], rhs=identF[:], start=True, stop=True)
+
             def x_words(h, gu):
                 bank = bank_tile("ps_x")
                 for i in range(4):
@@ -292,6 +302,8 @@ def tile_rwkv_timemix_pa_kernel(
 
             for v, vec in ((V_MUR, mu_r), (V_MUK, mu_k), (V_MUV, mu_v), (V_W, w), (V_U, u)):
                 nc.scalar.dma_start(out=sm[2 * v : 2 * v + 2, :], in_=vec.rearrange("(r c) -> r c", c=512))
+            warm = keep.tile([P, 1], F32)
+            nc.scalar.activation(out=warm[:], in_=epsT[:], func=AF.Exp)
             load_x(0, 2)
             nc.sync.dma_start(out=sm[2 * V_B0 : 2 * V_B0 + 8, :], in_=b0.rearrange("b (r c) -> (b r) c", c=512))
             nc.sync.dma_start(out=sm[2 * V_A0 : 2 * V_A0 + 8, :], in_=a0.rearrange("b (r c) -> (b r) c", c=512))
@@ -300,8 +312,9 @@ def tile_rwkv_timemix_pa_kernel(
                 w_load(s)
             load_x(1, 1)
 
+            for i in range(WARM0):
+                keep_warm()
             x_words(0, 0)
-            x_words(0, 1)
             ps_sm = bank_tile("ps_sm")
             for uu in range(2):
                 nc.tensor.transpose(ps_sm[:, P * uu : P * uu + P], sm[:].bitcast(F32)[:, uu:256:2], identF[:])
@@ -316,6 +329,10 @@ def tile_rwkv_timemix_pa_kernel(
             nc.vector.tensor_scalar_mul(out=negw[:], in0=sc[:, 8 * V_W : 8 * V_W + 8], scalar1=-1.0)
             difference_plane(VECTOR_UNITS[0])
             difference_plane(VECTOR_UNITS[1])
+            dec = gpool.tile([P, 8, T], F32, tag="gam", name="dec")
+            for m in range(8):
+                nc.scalar.activation(out=dec[:, m, :], in_=iota1[:], func=AF.Exp, scale=negw[:, m : m + 1])
+            x_words(0, 1)
             for mix in range(3):
                 for j in range(4):
                     mu = scal(V_MUR + mix, 4 * (TENSOR_GRP % 2) + j)
@@ -323,30 +340,38 @@ def tile_rwkv_timemix_pa_kernel(
                         nc.gpsimd.tensor_scalar(
                             out=diag[:, sign, mix, j, :], in0=eye[:], scalar1=mu, scalar2=0.0, op0=ALU.mult, op1=ALU.add
                         )
-            nc.vector.reciprocal(out=rb[:], in_=sc[:, 8 * V_B0 : 8 * V_B0 + 32])
-            nc.vector.tensor_tensor(out=alpha[:], in0=sc[:, 8 * V_A0 : 8 * V_A0 + 32], in1=rb[:], op=ALU.mult)
 
-            dec = gpool.tile([P, 8, T], F32, tag="gam", name="dec")
-            for m in range(8):
-                nc.scalar.activation(out=dec[:, m, :], in_=iota1[:], func=AF.Exp, scale=negw[:, m : m + 1])
             to_quantise = {n: [] for n in range(14)}
-            t_next = 0
+            w_quants = {n: [] for n in range(15)}
+            t_next = w_done = 0
             for n in range(12):
                 if n + 2 < 12:
                     difference_plane(VECTOR_UNITS[n + 2])
+                for i in range(WARM[n]):
+                    keep_warm()
                 for h, gu in X_STEPS.get(n, ()):
                     x_words(h, gu)
-                banks = [w_transposes(n, g) for g in range(2)] if n < W_FIRST else []
-                if banks:
-                    w_load(n + 3)
+                w_banks = []
+                for i in range(W_STEPS[n]):
+                    w_banks.append((w_done, [w_transposes(w_done, g) for g in range(2)]))
+                    w_load(w_done + 3)
+                    w_done += 1
+                if n == 5:
+                    nc.vector.reciprocal(out=rb[:], in_=sc[:, 8 * V_B0 : 8 * V_B0 + 32])
+                if n == 7:
+                    nc.vector.tensor_tensor(
+                        out=alpha[:], in0=sc[:, 8 * V_A0 : 8 * V_A0 + 32], in1=rb[:], op=ALU.mult
+                    )
                 if n == 6:
                     nc.vector.tensor_scalar_add(out=gbias[:], in0=gbias[:], scalar1=-math.log(EPS))
                 t_banks = []
                 for i in range(T_STEPS[n]):
                     t_banks.append((t_next, t_mix(t_next // 4, t_next % 4)))
                     t_next += 1
-                for g in range(len(banks)):
-                    w_evac(n, g, banks[g])
+                for tile, banks in w_banks:
+                    for g in range(2):
+                        w_evac(tile, g, banks[g])
+                    w_quants[n + W_LAG].append(tile)
                 for t, bank in t_banks:
                     t_evac(t // 4, t % 4, bank)
                     if t % 4 == 3:
@@ -360,13 +385,13 @@ def tile_rwkv_timemix_pa_kernel(
                 for j in TABLE0.get(n, ()):
                     sigmoid_table(0, j)
                 mix_plane(VECTOR_UNITS[n])
-                if 0 < n <= W_FIRST:
-                    w_quant(n - 1)
+                for tile in w_quants[n]:
+                    w_quant(tile)
                 for item in to_quantise[n]:
                     quantise_mix(item)
                 for grp, mix in V_REGROUPS.get(n, ()):
                     to_quantise[n + 1].append(regroup(grp, mix, 2))
-            return [lambda item=item: quantise_mix(item) for item in to_quantise[12] + to_quantise[13]]
+            return [lambda tile=tile: w_quant(tile) for tile in w_quants[12] + w_quants[13]] + [lambda item=item: quantise_mix(item) for item in to_quantise[12] + to_quantise[13]]
 
         def stages(pb, late):
             acc, ygrp, wgrp, rgrp, ots, held = {}, {}, {}, {}, {}, {}
@@ -482,6 +507,12 @@ def tile_rwkv_timemix_pa_kernel(
                     stop=(g == 1),
                 )
 
+            def stage2_tile(h, n):
+                ps = bank_tile("ps_s2")
+                stage2_pass(h, n, 0, ps)
+                stage2_pass(h, n, 1, ps)
+                stage2_out(h, n, ps, True)
+
             def stage2_out(h, n, ps, on_scalar):
                 tt, oh = n // 2, n % 2
                 t0 = HALF * h + P * tt
@@ -499,7 +530,12 @@ def tile_rwkv_timemix_pa_kernel(
             last_regroup = {}
             def do_regroup(mix):
                 last_regroup[mix] = regroup(2, mix, 2)
-            late = late + [lambda: do_regroup(0), lambda: do_regroup(1), lambda: quantise_mix(last_regroup[0]), lambda: do_regroup(2), lambda: quantise_mix(last_regroup[1]), lambda: quantise_mix(last_regroup[2])]
+            late = late + [lambda: do_regroup(0), lambda: do_regroup(1), lambda: quantise_mix(last_regroup[0])]
+            if not S_LATE:
+                late += [lambda: do_regroup(2)]
+            late += [lambda: quantise_mix(last_regroup[1])]
+            if not S_LATE:
+                late += [lambda: quantise_mix(last_regroup[2])]
             for un in range(4):
                 stage1_matmuls(un)
                 if w_next < 12:
@@ -532,6 +568,11 @@ def tile_rwkv_timemix_pa_kernel(
                         group_step(grp, k)
                         if k == 0:
                             subtract_v(un)
+                    if grp == 0 and S_LATE:
+                        if k == S_LATE[0]:
+                            last_regroup[2] = regroup(2, 2, 1)
+                        if k == S_LATE[1]:
+                            quantise_mix(last_regroup[2])
                     if grp == 0:
                         banks = [w_transposes(12 + k, g) for g in range(2)]
                         if k == 0:
@@ -543,13 +584,11 @@ def tile_rwkv_timemix_pa_kernel(
                         w_quant(15)
                     if grp < 2:
                         sigmoid_table(grp + 2, k)
-                    if grp == 2:
-                        for n in (2 * k, 2 * k + 1):
-                            ps = bank_tile("ps_s2")
-                            stage2_pass(0, n, 0, ps)
-                            stage2_pass(0, n, 1, ps)
-                            stage2_out(0, n, ps, True)
+                    if grp == 2 and k >= 4 - S2_EARLY:
+                        stage2_tile(0, k - 4 + S2_EARLY)
                     if grp == 3 and k == 0:
+                        for n in range(S2_EARLY, 8):
+                            stage2_tile(0, n)
                         for n in range(8):
                             open_banks.append(bank_tile("ps_s2"))
                             stage2_pass(1, n, 0, open_banks[n])
@@ -573,12 +612,12 @@ def tile_rwkv_timemix_pa_kernel(
             first = gate(3, 0, half_t)
             subtract_part(half_t, HALF)
             quantise_h(3, 0, half_t, first)
-            finish((0, 1, 2, 3), ())
+            finish((0, 1, 2), ())
             second = gate(3, half_t, last_t)
             third = gate(3, last_t, HALF)
             quantise_h(3, half_t, last_t, second)
             quantise_h(3, last_t, HALF, third)
-            finish((4, 5, 6, 7), (5, 7))
+            finish((3, 4, 5, 6, 7), (3, 5, 7))
 
         with tc.manual_schedule():
             with tc.tile_pool(name="pa", bufs=2) as pool_a:

@@ -22,16 +22,16 @@ FLOPS = 4 * 2 * NTOK * C * C
 
 TENSOR_GRP = 3
 W_FIRST = 8
-S2_EARLY = 4
-WARM0 = 0
-WARM = (0, 0, 0, 0, 0, 0, 0, 0, 0, 0, 0, 0)
+G_MULT = False
+PQ = (2, 3)
+S2_EARLY = 2
 W_LAG = 1
 W_STEPS = (0, 0, 0, 1, 1, 1, 1, 1, 1, 1, 1, 0)
 S_LATE = (0, 2)
 TABLE0 = {9: (0,), 10: (1, 2), 11: (3,)}
 LATE = (2, 2, 3, 3)
 X_VECTOR = ((0, 0),)
-S_MULT = (3,)
+S_MULT = ()
 X_STEPS = {1: ((0, 2),), 2: ((0, 3),), 3: ((1, 2),), 4: ((1, 3),), 5: ((1, 0),), 6: ((1, 1),)}
 T_STEPS = (0, 0, 0, 0, 0, 1, 1, 2, 2, 2, 2, 2)
 LN_ROWS = (0, 4, 8, 12, 16, 20, 24, 28, 32, 32, 32, 32, 32)
@@ -73,6 +73,7 @@ def tile_rwkv_timemix_pa_kernel(
         )
         sc = keep.tile([P, 160], F32)
         negw = keep.tile([P, 8], F32)
+        negu = keep.tile([P, 8], F32)
         rb = keep.tile([P, 32], F32)
         alpha = keep.tile([P, 32], F32)
         gbias = keep.tile([P, 32], F32)
@@ -106,12 +107,22 @@ def tile_rwkv_timemix_pa_kernel(
                 )
             for bb in range(2 if grp in S_MULT else 0):
                 m, b = 4 * g + j, 2 * h + bb
-                nc.scalar.activation(
-                    out=gam[grp][:, j, T * bb : T * bb + T],
-                    in_=gam[grp][:, j, T * bb : T * bb + T],
-                    func=AF.Copy,
-                    scale=alpha[:, 8 * b + m : 8 * b + m + 1],
-                )
+                if G_MULT:
+                    nc.gpsimd.tensor_scalar(
+                        out=gam[grp][:, j, T * bb : T * bb + T],
+                        in0=gam[grp][:, j, T * bb : T * bb + T],
+                        scalar1=alpha[:, 8 * b + m : 8 * b + m + 1],
+                        scalar2=0.0,
+                        op0=ALU.mult,
+                        op1=ALU.add,
+                    )
+                else:
+                    nc.scalar.activation(
+                        out=gam[grp][:, j, T * bb : T * bb + T],
+                        in_=gam[grp][:, j, T * bb : T * bb + T],
+                        func=AF.Copy,
+                        scale=alpha[:, 8 * b + m : 8 * b + m + 1],
+                    )
 
         wnat, wgt = {}, {}
 
@@ -216,10 +227,6 @@ def tile_rwkv_timemix_pa_kernel(
                     cs = slice(width * n, width * n + width)
                     nc.sync.dma_start(out=x_t[:, :, cs], in_=rows[:, cs].rearrange("(i p) c -> p i c", p=P))
 
-            def keep_warm():
-                bank = bank_tile("ps_warm")
-                nc.tensor.matmul(bank[:, 0:P], lhsT=identF[:], rhs=identF[:], start=True, stop=True)
-
             def x_words(h, gu):
                 bank = bank_tile("ps_x")
                 for i in range(4):
@@ -280,7 +287,7 @@ def tile_rwkv_timemix_pa_kernel(
                 gu, e, j, grp = m // 2, m % 2, m % 4, s // 4
                 if j == 0:
                     planes[grp] = [
-                        mid.tile([P, 4, HALF], BF16, tag="planes", bufs=6, name="planes%d" % i) for i in range(3)
+                        mid.tile([P, 4, HALF], BF16, tag="planes", bufs=4, name="planes%d" % i) for i in range(3)
                     ]
                 shifted = xw[:, gu, 2 * h : 2 * h + 2, 0:T].bitcast(BF16).rearrange("p b (t e) -> p b t e", e=2)[:, :, :, e]
                 for mix in range(3):
@@ -312,8 +319,6 @@ def tile_rwkv_timemix_pa_kernel(
                 w_load(s)
             load_x(1, 1)
 
-            for i in range(WARM0):
-                keep_warm()
             x_words(0, 0)
             ps_sm = bank_tile("ps_sm")
             for uu in range(2):
@@ -347,8 +352,6 @@ def tile_rwkv_timemix_pa_kernel(
             for n in range(12):
                 if n + 2 < 12:
                     difference_plane(VECTOR_UNITS[n + 2])
-                for i in range(WARM[n]):
-                    keep_warm()
                 for h, gu in X_STEPS.get(n, ()):
                     x_words(h, gu)
                 w_banks = []
@@ -356,6 +359,8 @@ def tile_rwkv_timemix_pa_kernel(
                     w_banks.append((w_done, [w_transposes(w_done, g) for g in range(2)]))
                     w_load(w_done + 3)
                     w_done += 1
+                if n == 4:
+                    nc.vector.tensor_scalar_mul(out=negu[:], in0=sc[:, 8 * V_U : 8 * V_U + 8], scalar1=-1.0)
                 if n == 5:
                     nc.vector.reciprocal(out=rb[:], in_=sc[:, 8 * V_B0 : 8 * V_B0 + 32])
                 if n == 7:
@@ -438,16 +443,31 @@ def tile_rwkv_timemix_pa_kernel(
                 j, grp = un % 4, un // 4
                 tok = slice(HALF * h, HALF * h + HALF)
                 if j == 0:
-                    ygrp[grp] = pb.tile([P, 4, HALF], F32, tag="grp", bufs=5, name="ygrp")
-                    wgrp[grp] = pb.tile([P, 4, HALF], F32, tag="grp", bufs=5, name="wgrp")
-                    rgrp[grp] = pb.tile([P, 4, HALF], F32, tag="grp", bufs=5, name="rgrp")
+                    ygrp[grp] = pb.tile([P, 4, HALF], F32, tag="grp", bufs=6, name="ygrp")
+                    wgrp[grp] = pb.tile([P, 4, HALF], F32, tag="grp", bufs=6, name="wgrp")
+                    rgrp[grp] = pb.tile([P, 4, HALF], F32, tag="grp", bufs=6, name="rgrp")
                 y_t = ygrp[grp][:, j, :]
                 nc.vector.tensor_tensor(out=y_t, in0=acc[(un, 1)][:], in1=q[:, m, tok], op=ALU.subtract)
-                nc.scalar.activation(out=y_t, in_=y_t, func=AF.Sigmoid, bias=scal(V_U, m))
+                if grp in PQ:
+                    nc.scalar.activation(out=wgrp[grp][:, j, :], in_=y_t, func=AF.Sigmoid, bias=scal(V_U, m))
+                    nc.scalar.activation(out=y_t, in_=y_t, func=AF.Sigmoid, scale=-1.0, bias=negu[:, m : m + 1])
+                    pieces = 2 if un == 15 else 1
+                    for i in range(pieces):
+                        cols = slice(HALF // pieces * i, HALF // pieces * (i + 1))
+                        nc.gpsimd.tensor_tensor(
+                            out=y_t[:, cols], in0=gam[grp][:, j, cols], in1=y_t[:, cols], op=ALU.mult
+                        )
+                else:
+                    nc.scalar.activation(out=y_t, in_=y_t, func=AF.Sigmoid, bias=scal(V_U, m))
                 nc.scalar.activation(out=rgrp[grp][:, j, :], in_=acc[(un, 0)][:], func=AF.Sigmoid)
 
             def subtract_v(un):
                 j, grp = un % 4, un // 4
+                if grp in PQ:
+                    nc.vector.tensor_tensor(
+                        out=wgrp[grp][:, j, :], in0=acc[(un, 2)][:], in1=wgrp[grp][:, j, :], op=ALU.mult
+                    )
+                    return
                 if grp in S_MULT:
                     nc.vector.tensor_tensor(
                         out=wgrp[grp][:, j, :], in0=gam[grp][:, j, :], in1=acc[(un, 2)][:], op=ALU.subtract
@@ -476,8 +496,31 @@ def tile_rwkv_timemix_pa_kernel(
                     in_=grouped[:].rearrange("p t j -> p (t j)"),
                 )
 
+            def add_parts(grp, lo, hi):
+                if grp in S_MULT:
+                    part = wgrp[grp][:, :, lo:hi]
+                    nc.vector.tensor_tensor(out=part, in0=part, in1=ygrp[grp][:, :, lo:hi], op=ALU.add)
+                else:
+                    h, g = grp // 2, grp % 2
+                    for bb in range(lo // T, hi // T):
+                        cols = slice(T * bb, T * bb + T)
+                        for j in range(4):
+                            m, b = 4 * g + j, 2 * h + bb
+                            nc.vector.scalar_tensor_tensor(
+                                out=wgrp[grp][:, j, cols],
+                                in0=ygrp[grp][:, j, cols],
+                                scalar=alpha[:, 8 * b + m : 8 * b + m + 1],
+                                in1=wgrp[grp][:, j, cols],
+                                op0=ALU.mult,
+                                op1=ALU.add,
+                            )
+
             def group_step(grp, k):
                 h, g = grp // 2, grp % 2
+                if grp in PQ and k < 2:
+                    if k == 1:
+                        add_parts(grp, 0, HALF)
+                    return
                 if k == 0:
                     nc.vector.tensor_tensor(out=flat(wgrp[grp]), in0=flat(wgrp[grp]), in1=flat(ygrp[grp]), op=ALU.mult)
                 elif k == 1:
@@ -517,7 +560,7 @@ def tile_rwkv_timemix_pa_kernel(
                 tt, oh = n // 2, n % 2
                 t0 = HALF * h + P * tt
                 if oh == 0:
-                    ots[h] = mid.tile([P, C], F32, tag="planes", bufs=6, name="ot")
+                    ots[h] = mid.tile([P, C], F32, tag="planes", bufs=4, name="ot")
                 dst = ots[h][:, HALF * oh : HALF * oh + HALF]
                 if on_scalar:
                     nc.scalar.copy(out=dst, in_=ps[:])
@@ -563,11 +606,16 @@ def tile_rwkv_timemix_pa_kernel(
                         un = 4 * grp + 4 + k
                         stage1_matmuls(un)
                         sigmoids(un)
-                        if k > 0:
-                            subtract_v(un)
-                        group_step(grp, k)
-                        if k == 0:
-                            subtract_v(un)
+                        if un // 4 in PQ:
+                            if un > 4 * PQ[0]:
+                                subtract_v(un - 1)
+                            group_step(grp, k)
+                        else:
+                            if k > 0:
+                                subtract_v(un)
+                            group_step(grp, k)
+                            if k == 0:
+                                subtract_v(un)
                     if grp == 0 and S_LATE:
                         if k == S_LATE[0]:
                             last_regroup[2] = regroup(2, 2, 1)
@@ -592,25 +640,16 @@ def tile_rwkv_timemix_pa_kernel(
                         for n in range(8):
                             open_banks.append(bank_tile("ps_s2"))
                             stage2_pass(1, n, 0, open_banks[n])
-            def multiply_part(lo, hi):
-                part = wgrp[3][:, :, lo:hi]
-                nc.vector.tensor_tensor(out=part, in0=part, in1=ygrp[3][:, :, lo:hi], op=ALU.mult)
-
-            def subtract_part(lo, hi):
-                part = wgrp[3][:, :, lo:hi]
-                nc.vector.tensor_tensor(out=part, in0=gam[3][:, :, lo:hi], in1=part, op=ALU.subtract)
-
             def finish(tiles, on_vector):
                 for n in tiles:
                     stage2_pass(1, n, 1, open_banks[n])
                     stage2_out(1, n, open_banks[n], n not in on_vector)
 
             half_t, last_t = T, T + P
-            multiply_part(0, half_t)
-            subtract_part(0, half_t)
-            multiply_part(half_t, HALF)
+            subtract_v(15)
+            add_parts(3, 0, half_t)
+            add_parts(3, half_t, HALF)
             first = gate(3, 0, half_t)
-            subtract_part(half_t, HALF)
             quantise_h(3, 0, half_t, first)
             finish((0, 1, 2), ())
             second = gate(3, half_t, last_t)

@@ -22,12 +22,15 @@ FLOPS = 4 * 2 * NTOK * C * C
 
 TENSOR_GRP = 3
 W_FIRST = 8
+SM_FIRST = True
+V_Q = 15
+W_OUT = (0, 1, 2, 3)
 G_MULT = False
-PQ = (2, 3)
+PQ = (1, 2, 3)
 S2_EARLY = 2
 W_LAG = 1
 W_STEPS = (0, 0, 0, 1, 1, 1, 1, 1, 1, 1, 1, 0)
-S_LATE = (0, 2)
+S_LATE = {1: 2}
 TABLE0 = {9: (0,), 10: (1, 2), 11: (3,)}
 LATE = (2, 2, 3, 3)
 X_VECTOR = ((0, 0),)
@@ -36,10 +39,10 @@ X_STEPS = {1: ((0, 2),), 2: ((0, 3),), 3: ((1, 2),), 4: ((1, 3),), 5: ((1, 0),),
 T_STEPS = (0, 0, 0, 0, 0, 1, 1, 2, 2, 2, 2, 2)
 LN_ROWS = (0, 4, 8, 12, 16, 20, 24, 28, 32, 32, 32, 32, 32)
 S_REGROUPS = {}
-V_REGROUPS = {3: ((0, 0), (0, 1), (0, 2)), 7: ((1, 0), (1, 1), (1, 2))}
+V_REGROUPS = {3: ((0, 0), (0, 1), (0, 2)), 7: ((1, 0), (1, 1)), 8: ((1, 2),)}
 VECTOR_UNITS = tuple(un for un in range(16) if un // 4 != TENSOR_GRP)
 
-V_W, V_U, V_MUR, V_MUK, V_MUV, V_A0, V_B0, V_XP = 0, 1, 2, 3, 4, 5, 9, 13
+V_MUR, V_MUK, V_MUV, V_XP, V_W, V_U, V_A0, V_B0 = 0, 1, 2, 3, 7, 8, 10, 14
 
 
 def tile_rwkv_timemix_pa_kernel(
@@ -51,7 +54,7 @@ def tile_rwkv_timemix_pa_kernel(
     weights = (W_r, W_k, W_v, W_out)
     with ExitStack() as ctx:
         keep = ctx.enter_context(tc.tile_pool(name="keep", bufs=1))
-        gpool = ctx.enter_context(tc.tile_pool(name="gpool", bufs=3))
+        gpool = ctx.enter_context(tc.tile_pool(name="gpool", bufs=2))
         wpool = ctx.enter_context(tc.tile_pool(name="wpool", bufs=2))
         mid = ctx.enter_context(tc.tile_pool(name="mid", bufs=4))
         psum = ctx.enter_context(tc.psum_pool(name="psum", bufs=8))
@@ -71,7 +74,7 @@ def tile_rwkv_timemix_pa_kernel(
         nc.gpsimd.iota(
             iota1[:], pattern=[[1, T]], base=1, channel_multiplier=0, allow_small_or_imprecise_dtypes=True
         )
-        sc = keep.tile([P, 160], F32)
+        sc = keep.tile([P, 144], F32)
         negw = keep.tile([P, 8], F32)
         negu = keep.tile([P, 8], F32)
         rb = keep.tile([P, 32], F32)
@@ -178,7 +181,7 @@ def tile_rwkv_timemix_pa_kernel(
         planes = {}
 
         def regroup(grp, mix, engine):
-            grouped = mid.tile([P, HALF, 4], BF16, tag="grouped", bufs=4, align_bytes=64, name="grouped")
+            grouped = mid.tile([P, HALF, 4], BF16, tag="grouped", bufs=5, align_bytes=64, name="grouped")
             dst = grouped[:].rearrange("p (c i) j -> p c j i", i=4)
             src = planes[grp][mix][:].rearrange("p j (c i) -> p c j i", i=4)
             if engine == 0:
@@ -208,12 +211,14 @@ def tile_rwkv_timemix_pa_kernel(
 
         def mixes_and_weights(pa):
             sm = pa.tile([P, 512], BF16, bufs=1, name="sm")
-            nc.vector.memset(sm[32:64, :], 0.0)
-            nc.vector.memset(sm[64:P, :], 0.0)
+            sm2 = pa.tile([P, 512], BF16, bufs=1, name="sm2")
+            for tile in (sm, sm2):
+                nc.vector.memset(tile[32:64, :], 0.0)
+                nc.vector.memset(tile[64:P, :], 0.0)
             diffB = pa.tile([P, P], BF16, bufs=1, name="diffB")
             nc.vector.tensor_copy(out=diffB[:, 0:1], in_=identB[:, 0:1])
             nc.vector.tensor_tensor(out=diffB[:, 1:P], in0=identB[:, 1:P], in1=identB[:, 0 : P - 1], op=ALU.subtract)
-            smt = pa.tile([P, 40, 2], F32, bufs=1, name="smt")
+            smt = pa.tile([P, 36, 2], F32, bufs=1, name="smt")
             x_nat, dbank, t_grouped = {}, {}, {}
             diag = pa.tile([P, 2, 3, 4, P], BF16, bufs=1, name="diag")
             xw = pa.tile([P, 4, 4, T + 1], F32, bufs=1, name="xw")
@@ -257,7 +262,7 @@ def tile_rwkv_timemix_pa_kernel(
 
             def t_evac(mix, i, bank):
                 if i == 0:
-                    t_grouped[mix] = mid.tile([P, HALF, 4], BF16, tag="grouped", bufs=4, align_bytes=64, name="t_grouped")
+                    t_grouped[mix] = mid.tile([P, HALF, 4], BF16, tag="grouped", bufs=5, align_bytes=64, name="t_grouped")
                 nc.scalar.copy(
                     out=t_grouped[mix][:, P * i : P * i + P, :], in_=bank[:].rearrange("p (j t) -> p t j", j=4)
                 )
@@ -287,7 +292,7 @@ def tile_rwkv_timemix_pa_kernel(
                 gu, e, j, grp = m // 2, m % 2, m % 4, s // 4
                 if j == 0:
                     planes[grp] = [
-                        mid.tile([P, 4, HALF], BF16, tag="planes", bufs=4, name="planes%d" % i) for i in range(3)
+                        mid.tile([P, 4, HALF], BF16, tag="planes", bufs=5, name="planes%d" % i) for i in range(3)
                     ]
                 shifted = xw[:, gu, 2 * h : 2 * h + 2, 0:T].bitcast(BF16).rearrange("p b (t e) -> p b t e", e=2)[:, :, :, e]
                 for mix in range(3):
@@ -309,24 +314,36 @@ def tile_rwkv_timemix_pa_kernel(
 
             for v, vec in ((V_MUR, mu_r), (V_MUK, mu_k), (V_MUV, mu_v), (V_W, w), (V_U, u)):
                 nc.scalar.dma_start(out=sm[2 * v : 2 * v + 2, :], in_=vec.rearrange("(r c) -> r c", c=512))
+            nc.scalar.dma_start(out=sm[2 * V_XP : 2 * V_XP + 8, :], in_=x_prev0.rearrange("b (r c) -> (b r) c", c=512))
+            nc.scalar.dma_start(out=sm[18:32, :], in_=x_flat[0:14, 0:512])
             warm = keep.tile([P, 1], F32)
             nc.scalar.activation(out=warm[:], in_=epsT[:], func=AF.Exp)
             load_x(0, 2)
-            nc.sync.dma_start(out=sm[2 * V_B0 : 2 * V_B0 + 8, :], in_=b0.rearrange("b (r c) -> (b r) c", c=512))
-            nc.sync.dma_start(out=sm[2 * V_A0 : 2 * V_A0 + 8, :], in_=a0.rearrange("b (r c) -> (b r) c", c=512))
-            nc.sync.dma_start(out=sm[2 * V_XP : 2 * V_XP + 8, :], in_=x_prev0.rearrange("b (r c) -> (b r) c", c=512))
+            nc.sync.dma_start(out=sm2[0:8, :], in_=a0.rearrange("b (r c) -> (b r) c", c=512))
+            nc.sync.dma_start(out=sm2[8:16, :], in_=b0.rearrange("b (r c) -> (b r) c", c=512))
+            nc.sync.dma_start(out=sm2[16:32, :], in_=x_flat[0:16, 0:512])
             for s in range(3):
                 w_load(s)
             load_x(1, 1)
 
-            x_words(0, 0)
-            ps_sm = bank_tile("ps_sm")
-            for uu in range(2):
-                nc.tensor.transpose(ps_sm[:, P * uu : P * uu + P], sm[:].bitcast(F32)[:, uu:256:2], identF[:])
-            nc.vector.tensor_copy(
-                out=smt[:], in_=ps_sm[:, 0:256].rearrange("p (u r) -> p r u", u=2)[:, 0:40, :]
-            )
-            nc.vector.tensor_copy(out=sc[:], in_=smt[:].rearrange("p r u -> p (r u)").bitcast(BF16))
+            def vector_words(tile, first, rows):
+                bank = bank_tile("ps_sm")
+                for uu in range(2):
+                    nc.tensor.transpose(bank[:, P * uu : P * uu + P], tile[:].bitcast(F32)[:, uu:256:2], identF[:])
+                words = smt[:, first : first + rows, :]
+                nc.vector.tensor_copy(
+                    out=words, in_=bank[:, 0:256].rearrange("p (u r) -> p r u", u=2)[:, 0:rows, :]
+                )
+                nc.vector.tensor_copy(
+                    out=sc[:, 4 * first : 4 * first + 4 * rows], in_=words.rearrange("p r u -> p (r u)").bitcast(BF16)
+                )
+
+            if SM_FIRST:
+                vector_words(sm, 0, 20)
+                x_words(0, 0)
+            else:
+                x_words(0, 0)
+                vector_words(sm, 0, 20)
             nc.vector.tensor_copy(
                 out=xw[:, :, :, 0].rearrange("p (g u) b -> p g u b", u=2),
                 in_=smt[:, 2 * V_XP : 2 * V_XP + 8, :].rearrange("p (b g) u -> p g u b", g=2),
@@ -334,6 +351,8 @@ def tile_rwkv_timemix_pa_kernel(
             nc.vector.tensor_scalar_mul(out=negw[:], in0=sc[:, 8 * V_W : 8 * V_W + 8], scalar1=-1.0)
             difference_plane(VECTOR_UNITS[0])
             difference_plane(VECTOR_UNITS[1])
+            mix_plane(VECTOR_UNITS[0])
+            vector_words(sm2, 20, 16)
             dec = gpool.tile([P, 8, T], F32, tag="gam", name="dec")
             for m in range(8):
                 nc.scalar.activation(out=dec[:, m, :], in_=iota1[:], func=AF.Exp, scale=negw[:, m : m + 1])
@@ -389,7 +408,8 @@ def tile_rwkv_timemix_pa_kernel(
                     to_quantise[n + 2].append(regroup(grp, mix, 1))
                 for j in TABLE0.get(n, ()):
                     sigmoid_table(0, j)
-                mix_plane(VECTOR_UNITS[n])
+                if n > 0:
+                    mix_plane(VECTOR_UNITS[n])
                 for tile in w_quants[n]:
                     w_quant(tile)
                 for item in to_quantise[n]:
@@ -451,12 +471,8 @@ def tile_rwkv_timemix_pa_kernel(
                 if grp in PQ:
                     nc.scalar.activation(out=wgrp[grp][:, j, :], in_=y_t, func=AF.Sigmoid, bias=scal(V_U, m))
                     nc.scalar.activation(out=y_t, in_=y_t, func=AF.Sigmoid, scale=-1.0, bias=negu[:, m : m + 1])
-                    pieces = 2 if un == 15 else 1
-                    for i in range(pieces):
-                        cols = slice(HALF // pieces * i, HALF // pieces * (i + 1))
-                        nc.gpsimd.tensor_tensor(
-                            out=y_t[:, cols], in0=gam[grp][:, j, cols], in1=y_t[:, cols], op=ALU.mult
-                        )
+                    if un < V_Q:
+                        nc.gpsimd.tensor_tensor(out=y_t, in0=gam[grp][:, j, :], in1=y_t, op=ALU.mult)
                 else:
                     nc.scalar.activation(out=y_t, in_=y_t, func=AF.Sigmoid, bias=scal(V_U, m))
                 nc.scalar.activation(out=rgrp[grp][:, j, :], in_=acc[(un, 0)][:], func=AF.Sigmoid)
@@ -478,7 +494,7 @@ def tile_rwkv_timemix_pa_kernel(
 
             def gate(grp, lo, hi):
                 cols = slice(lo, hi)
-                grouped = mid.tile([P, hi - lo, 4], BF16, tag="grouped", bufs=4, align_bytes=64, name="grouped")
+                grouped = mid.tile([P, hi - lo, 4], BF16, tag="grouped", bufs=5, align_bytes=64, name="grouped")
                 nc.vector.tensor_tensor(
                     out=grouped[:].rearrange("p (c i) j -> p c j i", i=4),
                     in0=runs_of_four(wgrp[grp], cols),
@@ -560,27 +576,36 @@ def tile_rwkv_timemix_pa_kernel(
                 tt, oh = n // 2, n % 2
                 t0 = HALF * h + P * tt
                 if oh == 0:
-                    ots[h] = mid.tile([P, C], F32, tag="planes", bufs=4, name="ot")
+                    ots[h] = mid.tile([P, C], F32, tag="planes", bufs=5, name="ot")
                 dst = ots[h][:, HALF * oh : HALF * oh + HALF]
                 if on_scalar:
                     nc.scalar.copy(out=dst, in_=ps[:])
                 else:
                     nc.vector.tensor_copy(out=dst, in_=ps[:])
-                if oh == 1:
+                if n >= 4 and h == 1:
+                    cols = slice(HALF * oh, HALF * oh + HALF)
+                    nc.sync.dma_start(out=out_flat[t0 : t0 + P, cols], in_=ots[h][:, cols])
+                elif oh == 1:
                     nc.sync.dma_start(out=out_flat[t0 : t0 + P, :], in_=ots[h][:])
 
             w_next = W_FIRST
             last_regroup = {}
-            def do_regroup(mix):
-                last_regroup[mix] = regroup(2, mix, 2)
-            late = late + [lambda: do_regroup(0), lambda: do_regroup(1), lambda: quantise_mix(last_regroup[0])]
-            if not S_LATE:
-                late += [lambda: do_regroup(2)]
-            late += [lambda: quantise_mix(last_regroup[1])]
-            if not S_LATE:
-                late += [lambda: quantise_mix(last_regroup[2])]
+            def do_regroup(mix, engine):
+                last_regroup[mix] = regroup(2, mix, engine)
+
+            v_mixes = [mix for mix in range(3) if mix not in S_LATE.values()]
+            for mix in v_mixes:
+                late.append(lambda mix=mix: do_regroup(mix, 2))
+            for mix in v_mixes + list(S_LATE.values()):
+                late.append(lambda mix=mix: quantise_mix(last_regroup[mix]))
+            def next_place(un):
+                if 3 <= un < 15:
+                    sigmoid_table((un + 1) // 4, (un + 1) % 4)
+
             for un in range(4):
                 stage1_matmuls(un)
+                if un in S_LATE:
+                    do_regroup(S_LATE[un], 1)
                 if w_next < 12:
                     banks = [w_transposes(w_next, g) for g in range(2)]
                     if w_next + 3 < 16:
@@ -598,7 +623,7 @@ def tile_rwkv_timemix_pa_kernel(
                 for i in range(LATE[un]):
                     if late:
                         late.pop(0)()
-                sigmoid_table(1, un)
+                next_place(un)
             open_banks = []
             for grp in range(4):
                 for k in range(4):
@@ -616,22 +641,22 @@ def tile_rwkv_timemix_pa_kernel(
                             group_step(grp, k)
                             if k == 0:
                                 subtract_v(un)
-                    if grp == 0 and S_LATE:
-                        if k == S_LATE[0]:
-                            last_regroup[2] = regroup(2, 2, 1)
-                        if k == S_LATE[1]:
-                            quantise_mix(last_regroup[2])
-                    if grp == 0:
-                        banks = [w_transposes(12 + k, g) for g in range(2)]
-                        if k == 0:
+                    while late and grp == 0:
+                        late.pop(0)()
+                    bs = 4 * grp + k
+                    if bs == 0:
+                        w_quant(11)
+                    if bs in W_OUT:
+                        tile = 12 + W_OUT.index(bs)
+                        banks = [w_transposes(tile, g) for g in range(2)]
+                        if tile == 12:
                             w_load(15)
                         for g in range(2):
-                            w_evac(12 + k, g, banks[g])
-                        w_quant(11 + k)
-                    if grp == 1 and k == 0:
-                        w_quant(15)
-                    if grp < 2:
-                        sigmoid_table(grp + 2, k)
+                            w_evac(tile, g, banks[g])
+                    if bs - 1 in W_OUT:
+                        w_quant(12 + W_OUT.index(bs - 1))
+                    if grp < 3:
+                        next_place(4 * grp + 4 + k)
                     if grp == 2 and k >= 4 - S2_EARLY:
                         stage2_tile(0, k - 4 + S2_EARLY)
                     if grp == 3 and k == 0:
@@ -647,6 +672,9 @@ def tile_rwkv_timemix_pa_kernel(
 
             half_t, last_t = T, T + P
             subtract_v(15)
+            for un in range(V_Q, 16):
+                y_t = ygrp[3][:, un - 12, :]
+                nc.vector.tensor_tensor(out=y_t, in0=gam[3][:, un - 12, :], in1=y_t, op=ALU.mult)
             add_parts(3, 0, half_t)
             add_parts(3, half_t, HALF)
             first = gate(3, 0, half_t)

@@ -22,7 +22,7 @@ FLOPS = 4 * 2 * NTOK * C * C
 
 TENSOR_GRP = 3
 W_FIRST = 8
-SM_FIRST = True
+SM_FIRST = False
 V_Q = 15
 W_OUT = (0, 1, 2, 3)
 G_MULT = False
@@ -63,17 +63,10 @@ def tile_rwkv_timemix_pa_kernel(
             return psum.tile([P, HALF], F32, tag="ps", name=name)
 
         epsT = keep.tile([P, 1], F32)
-        nc.vector.memset(epsT[:], EPS)
         identF = keep.tile([P, P], F32)
-        make_identity(nc, identF[:])
         identB = keep.tile([P, P], BF16)
-        make_identity(nc, identB[:])
         negB = keep.tile([P, P], BF16)
-        nc.vector.tensor_scalar_mul(out=negB[:], in0=identB[:], scalar1=-1.0)
         iota1 = keep.tile([P, T], F32)
-        nc.gpsimd.iota(
-            iota1[:], pattern=[[1, T]], base=1, channel_multiplier=0, allow_small_or_imprecise_dtypes=True
-        )
         sc = keep.tile([P, 144], F32)
         negw = keep.tile([P, 8], F32)
         negu = keep.tile([P, 8], F32)
@@ -212,9 +205,15 @@ def tile_rwkv_timemix_pa_kernel(
         def mixes_and_weights(pa):
             sm = pa.tile([P, 512], BF16, bufs=1, name="sm")
             sm2 = pa.tile([P, 512], BF16, bufs=1, name="sm2")
-            for tile in (sm, sm2):
-                nc.vector.memset(tile[32:64, :], 0.0)
-                nc.vector.memset(tile[64:P, :], 0.0)
+            nc.vector.memset(sm[:], 0.0)
+            nc.vector.memset(epsT[:], EPS)
+            nc.vector.memset(sm2[:], 0.0)
+            make_identity(nc, identF[:])
+            make_identity(nc, identB[:])
+            nc.vector.tensor_scalar_mul(out=negB[:], in0=identB[:], scalar1=-1.0)
+            nc.gpsimd.iota(
+                iota1[:], pattern=[[1, T]], base=1, channel_multiplier=0, allow_small_or_imprecise_dtypes=True
+            )
             diffB = pa.tile([P, P], BF16, bufs=1, name="diffB")
             nc.vector.tensor_copy(out=diffB[:, 0:1], in_=identB[:, 0:1])
             nc.vector.tensor_tensor(out=diffB[:, 1:P], in0=identB[:, 1:P], in1=identB[:, 0 : P - 1], op=ALU.subtract)
@@ -223,14 +222,11 @@ def tile_rwkv_timemix_pa_kernel(
             diag = pa.tile([P, 2, 3, 4, P], BF16, bufs=1, name="diag")
             xw = pa.tile([P, 4, 4, T + 1], F32, bufs=1, name="xw")
 
-            def load_x(h, pieces):
-                x_t = pa.tile([P, 4, C], BF16, tag="xnat", bufs=2, name="x_nat")
-                x_nat[h] = x_t
-                rows = x_flat[HALF * h : HALF * h + HALF, :]
-                width = C // pieces
-                for n in range(pieces):
-                    cs = slice(width * n, width * n + width)
-                    nc.sync.dma_start(out=x_t[:, :, cs], in_=rows[:, cs].rearrange("(i p) c -> p i c", p=P))
+            def load_x(h, cs):
+                if h not in x_nat:
+                    x_nat[h] = pa.tile([P, 4, C], BF16, tag="xnat", bufs=2, name="x_nat")
+                rows = x_flat[HALF * h : HALF * h + HALF, cs]
+                nc.sync.dma_start(out=x_nat[h][:, :, cs], in_=rows.rearrange("(i p) c -> p i c", p=P))
 
             def x_words(h, gu):
                 bank = bank_tile("ps_x")
@@ -314,17 +310,16 @@ def tile_rwkv_timemix_pa_kernel(
 
             for v, vec in ((V_MUR, mu_r), (V_MUK, mu_k), (V_MUV, mu_v), (V_W, w), (V_U, u)):
                 nc.scalar.dma_start(out=sm[2 * v : 2 * v + 2, :], in_=vec.rearrange("(r c) -> r c", c=512))
-            nc.scalar.dma_start(out=sm[2 * V_XP : 2 * V_XP + 8, :], in_=x_prev0.rearrange("b (r c) -> (b r) c", c=512))
-            nc.scalar.dma_start(out=sm[18:32, :], in_=x_flat[0:14, 0:512])
             warm = keep.tile([P, 1], F32)
             nc.scalar.activation(out=warm[:], in_=epsT[:], func=AF.Exp)
-            load_x(0, 2)
-            nc.sync.dma_start(out=sm2[0:8, :], in_=a0.rearrange("b (r c) -> (b r) c", c=512))
+            load_x(0, slice(0, 512))
+            nc.sync.dma_start(out=sm[2 * V_XP : 2 * V_XP + 8, :], in_=x_prev0.rearrange("b (r c) -> (b r) c", c=512))
+            load_x(0, slice(512, C))
             nc.sync.dma_start(out=sm2[8:16, :], in_=b0.rearrange("b (r c) -> (b r) c", c=512))
-            nc.sync.dma_start(out=sm2[16:32, :], in_=x_flat[0:16, 0:512])
+            nc.sync.dma_start(out=sm2[0:8, :], in_=a0.rearrange("b (r c) -> (b r) c", c=512))
             for s in range(3):
                 w_load(s)
-            load_x(1, 1)
+            load_x(1, slice(0, C))
 
             def vector_words(tile, first, rows):
                 bank = bank_tile("ps_sm")

@@ -22,17 +22,20 @@ FLOPS = 4 * 2 * NTOK * C * C
 
 TENSOR_GRP = 3
 W_FIRST = 8
+PQ_LATE = False
+G_COLS = 448
+NEXT0 = 3
 SM_FIRST = False
 V_Q = 15
-W_OUT = (0, 1, 2, 3)
+W_OUT = (0, 2, 4, 6)
 G_MULT = False
 PQ = (1, 2, 3)
 S2_EARLY = 2
 W_LAG = 1
 W_STEPS = (0, 0, 0, 1, 1, 1, 1, 1, 1, 1, 1, 0)
 S_LATE = {1: 2}
-TABLE0 = {9: (0,), 10: (1, 2), 11: (3,)}
-LATE = (2, 2, 3, 3)
+TABLE0 = {8: (0,), 9: (1,), 10: (2,), 11: (3,)}
+LATE = (3, 2, 3, 3)
 X_VECTOR = ((0, 0),)
 S_MULT = ()
 X_STEPS = {1: ((0, 2),), 2: ((0, 3),), 3: ((1, 2),), 4: ((1, 3),), 5: ((1, 0),), 6: ((1, 1),)}
@@ -467,7 +470,10 @@ def tile_rwkv_timemix_pa_kernel(
                     nc.scalar.activation(out=wgrp[grp][:, j, :], in_=y_t, func=AF.Sigmoid, bias=scal(V_U, m))
                     nc.scalar.activation(out=y_t, in_=y_t, func=AF.Sigmoid, scale=-1.0, bias=negu[:, m : m + 1])
                     if un < V_Q:
-                        nc.gpsimd.tensor_tensor(out=y_t, in0=gam[grp][:, j, :], in1=y_t, op=ALU.mult)
+                        part = slice(0, G_COLS)
+                        nc.gpsimd.tensor_tensor(
+                            out=y_t[:, part], in0=gam[grp][:, j, part], in1=y_t[:, part], op=ALU.mult
+                        )
                 else:
                     nc.scalar.activation(out=y_t, in_=y_t, func=AF.Sigmoid, bias=scal(V_U, m))
                 nc.scalar.activation(out=rgrp[grp][:, j, :], in_=acc[(un, 0)][:], func=AF.Sigmoid)
@@ -529,6 +535,9 @@ def tile_rwkv_timemix_pa_kernel(
             def group_step(grp, k):
                 h, g = grp // 2, grp % 2
                 if grp in PQ and k < 2:
+                    if k == 0 and G_COLS < HALF:
+                        rest = ygrp[grp][:, :, G_COLS:HALF]
+                        nc.vector.tensor_tensor(out=rest, in0=gam[grp][:, :, G_COLS:HALF], in1=rest, op=ALU.mult)
                     if k == 1:
                         add_parts(grp, 0, HALF)
                     return
@@ -594,7 +603,7 @@ def tile_rwkv_timemix_pa_kernel(
             for mix in v_mixes + list(S_LATE.values()):
                 late.append(lambda mix=mix: quantise_mix(last_regroup[mix]))
             def next_place(un):
-                if 3 <= un < 15:
+                if NEXT0 <= un < 15:
                     sigmoid_table((un + 1) // 4, (un + 1) % 4)
 
             for un in range(4):
@@ -608,7 +617,10 @@ def tile_rwkv_timemix_pa_kernel(
                 else:
                     banks = []
                 sigmoids(un)
-                subtract_v(un)
+                if 0 not in PQ:
+                    subtract_v(un)
+                elif un > 0:
+                    subtract_v(un - 1)
                 for g in range(len(banks)):
                     w_evac(w_next, g, banks[g])
                 if w_next > W_FIRST:
@@ -629,7 +641,13 @@ def tile_rwkv_timemix_pa_kernel(
                         if un // 4 in PQ:
                             if un > 4 * PQ[0]:
                                 subtract_v(un - 1)
-                            group_step(grp, k)
+                            if PQ_LATE and grp in PQ:
+                                if k >= 2:
+                                    group_step(grp, k - 1)
+                                if k == 0 and grp - 1 in PQ:
+                                    group_step(grp - 1, 3)
+                            else:
+                                group_step(grp, k)
                         else:
                             if k > 0:
                                 subtract_v(un)
@@ -655,6 +673,8 @@ def tile_rwkv_timemix_pa_kernel(
                     if grp == 2 and k >= 4 - S2_EARLY:
                         stage2_tile(0, k - 4 + S2_EARLY)
                     if grp == 3 and k == 0:
+                        if PQ_LATE:
+                            group_step(2, 3)
                         for n in range(S2_EARLY, 8):
                             stage2_tile(0, n)
                         for n in range(8):
@@ -667,6 +687,9 @@ def tile_rwkv_timemix_pa_kernel(
 
             half_t, last_t = T, T + P
             subtract_v(15)
+            if G_COLS < HALF:
+                rest = ygrp[3][:, 0 : V_Q - 12, G_COLS:HALF]
+                nc.vector.tensor_tensor(out=rest, in0=gam[3][:, 0 : V_Q - 12, G_COLS:HALF], in1=rest, op=ALU.mult)
             for un in range(V_Q, 16):
                 y_t = ygrp[3][:, un - 12, :]
                 nc.vector.tensor_tensor(out=y_t, in0=gam[3][:, un - 12, :], in1=y_t, op=ALU.mult)

@@ -22,6 +22,7 @@ FLOPS = 4 * 2 * NTOK * C * C
 
 TENSOR_GRP = 3
 W_FIRST = 8
+G_RG = {4: ((0, 2, 0),), 5: ((0, 2, 1),), 8: ((1, 2, 0),), 9: ((1, 2, 1),)}
 PQ_LATE = False
 G_COLS = 448
 NEXT0 = 3
@@ -42,7 +43,7 @@ X_STEPS = {1: ((0, 2),), 2: ((0, 3),), 3: ((1, 2),), 4: ((1, 3),), 5: ((1, 0),),
 T_STEPS = (0, 0, 0, 0, 0, 1, 1, 2, 2, 2, 2, 2)
 LN_ROWS = (0, 4, 8, 12, 16, 20, 24, 28, 32, 32, 32, 32, 32)
 S_REGROUPS = {}
-V_REGROUPS = {3: ((0, 0), (0, 1), (0, 2)), 7: ((1, 0), (1, 1)), 8: ((1, 2),)}
+V_REGROUPS = {3: ((0, 0), (0, 1)), 7: ((1, 0), (1, 1))}
 VECTOR_UNITS = tuple(un for un in range(16) if un // 4 != TENSOR_GRP)
 
 V_MUR, V_MUK, V_MUV, V_XP, V_W, V_U, V_A0, V_B0 = 0, 1, 2, 3, 7, 8, 10, 14
@@ -194,6 +195,21 @@ def tile_rwkv_timemix_pa_kernel(
             else:
                 nc.vector.tensor_copy(out=dst, in_=src)
             return (grp, mix, grouped)
+
+        g_grouped = {}
+
+        def g_regroup(grp, mix, half, gate_one):
+            if half == 0:
+                g_grouped[(grp, mix)] = mid.tile([P, HALF, 4], BF16, tag="grouped", bufs=5, align_bytes=64, name="grouped")
+            tok = slice(T * half, T * half + T)
+            nc.gpsimd.tensor_scalar(
+                out=g_grouped[(grp, mix)][:, tok, :],
+                in0=planes[grp][mix][:, :, tok].rearrange("p j t -> p t j"),
+                scalar1=gate_one[:],
+                scalar2=0.0,
+                op0=ALU.mult,
+                op1=ALU.add,
+            )
 
         def quantise_mix(item):
             grp, mix, grouped = item
@@ -402,6 +418,10 @@ def tile_rwkv_timemix_pa_kernel(
                     nc.scalar.activation(out=gbias[:], in_=sc[:, 8 * V_B0 : 8 * V_B0 + 32], func=AF.Ln)
                 for row in range(LN_ROWS[n], LN_ROWS[n + 1]):
                     ln_table(row)
+                for grp, mix, half in G_RG.get(n, ()):
+                    g_regroup(grp, mix, half, gate_one)
+                    if half == 1:
+                        to_quantise[n + 1].append((grp, mix, g_grouped[(grp, mix)]))
                 for grp, mix in S_REGROUPS.get(n, ()):
                     to_quantise[n + 2].append(regroup(grp, mix, 1))
                 for j in TABLE0.get(n, ()):
@@ -414,6 +434,9 @@ def tile_rwkv_timemix_pa_kernel(
                     quantise_mix(item)
                 for grp, mix in V_REGROUPS.get(n, ()):
                     to_quantise[n + 1].append(regroup(grp, mix, 2))
+                if n + 1 in G_RG:
+                    gate_one = pa.tile([P, 1], F32, tag="gate", bufs=2, name="gate_one")
+                    nc.vector.memset(gate_one[:], 1.0)
             return [lambda tile=tile: w_quant(tile) for tile in w_quants[12] + w_quants[13]] + [lambda item=item: quantise_mix(item) for item in to_quantise[12] + to_quantise[13]]
 
         def stages(pb, late):

import math
from contextlib import ExitStack

import concourse.mybir as mybir
from concourse.masks import make_identity

F32 = mybir.dt.float32
BF16 = mybir.dt.bfloat16
U32 = mybir.dt.uint32
U8 = mybir.dt.uint8
FP8X4 = mybir.dt.float8_e4m3fn_x4
ALU = mybir.AluOpType
AF = mybir.ActivationFunctionType

P = 128
C = 1024
NTOK = 1024
T = 256
HALF = 512
EPS = 1e-8
FLOPS = 4 * 2 * NTOK * C * C

TENSOR_GRP = 3
W_FIRST = 8
G_RG = {4: ((0, 2, 0),), 5: ((0, 2, 1),), 8: ((1, 2, 0),), 9: ((1, 2, 1),)}
PQ_LATE = False
G_COLS = 448
NEXT0 = 3
SM_FIRST = False
V_Q = 15
W_OUT = (0, 2, 4, 6)
G_MULT = False
PQ = (1, 2, 3)
S2_EARLY = 2
W_LAG = 1
W_STEPS = (0, 0, 0, 1, 1, 1, 1, 1, 1, 1, 1, 0)
S_LATE = {1: 2}
TABLE0 = {8: (0,), 9: (1,), 10: (2,), 11: (3,)}
LATE = (3, 2, 3, 3)
X_VECTOR = ((0, 0),)
S_MULT = ()
X_STEPS = {1: ((0, 2),), 2: ((0, 3),), 3: ((1, 2),), 4: ((1, 3),), 5: ((1, 0),), 6: ((1, 1),)}
T_STEPS = (0, 0, 0, 0, 0, 1, 1, 2, 2, 2, 2, 2)
LN_ROWS = (0, 4, 8, 12, 16, 20, 24, 28, 32, 32, 32, 32, 32)
S_REGROUPS = {}
V_REGROUPS = {3: ((0, 0), (0, 1)), 7: ((1, 0), (1, 1))}
VECTOR_UNITS = tuple(un for un in range(16) if un // 4 != TENSOR_GRP)

V_MUR, V_MUK, V_MUV, V_XP, V_W, V_U, V_A0, V_B0 = 0, 1, 2, 3, 7, 8, 10, 14


def tile_rwkv_timemix_pa_kernel(
    tc, x, a0, b0, x_prev0, w, u, mu_r, mu_k, mu_v, W_r, W_k, W_v, W_out, out
):
    nc = tc.nc
    x_flat = x.flatten_outer_dims()
    out_flat = out.flatten_outer_dims()
    weights = (W_r, W_k, W_v, W_out)
    with ExitStack() as ctx:
        keep = ctx.enter_context(tc.tile_pool(name="keep", bufs=1))
        gpool = ctx.enter_context(tc.tile_pool(name="gpool", bufs=2))
        wpool = ctx.enter_context(tc.tile_pool(name="wpool", bufs=2))
        mid = ctx.enter_context(tc.tile_pool(name="mid", bufs=4))
        psum = ctx.enter_context(tc.psum_pool(name="psum", bufs=8))

        def bank_tile(name):
            return psum.tile([P, HALF], F32, tag="ps", name=name)

        epsT = keep.tile([P, 1], F32)
        identF = keep.tile([P, P], F32)
        identB = keep.tile([P, P], BF16)
        negB = keep.tile([P, P], BF16)
        iota1 = keep.tile([P, T], F32)
        sc = keep.tile([P, 144], F32)
        negw = keep.tile([P, 8], F32)
        negu = keep.tile([P, 8], F32)
        rb = keep.tile([P, 32], F32)
        alpha = keep.tile([P, 32], F32)
        gbias = keep.tile([P, 32], F32)

        def scal(v, m):
            return sc[:, 8 * v + m : 8 * v + m + 1]

        wc = [keep.tile([P, 4, 2, T], U32, align_bytes=64, name="wc%d" % i) for i in range(3)]
        ws = [keep.tile([P, 4, 2, T], U8, align_bytes=64, name="ws%d" % i) for i in range(3)]
        woc = keep.tile([P, 2, C], U32, align_bytes=64)
        wos = keep.tile([P, 2, C], U8, align_bytes=64)
        xc = [keep.tile([P, 2, NTOK], U32, align_bytes=64, name="xc%d" % i) for i in range(3)]
        xsc = [keep.tile([P, 2, NTOK], U8, align_bytes=64, name="xsc%d" % i) for i in range(3)]
        hc = keep.tile([P, 2, NTOK], U32, align_bytes=64)
        hs = keep.tile([P, 2, NTOK], U8, align_bytes=64)
        q = keep.tile([P, 8, NTOK], F32)
        gam = {}

        def sigmoid_table(grp, j):
            h, g = grp // 2, grp % 2
            if j == 0:
                gam[grp] = gpool.tile([P, 4, HALF], F32, tag="gam", name="gam")
            for bb in range(2):
                m, b = 4 * g + j, 2 * h + bb
                nc.scalar.activation(
                    out=gam[grp][:, j, T * bb : T * bb + T],
                    in_=iota1[:],
                    func=AF.Sigmoid,
                    scale=negw[:, m : m + 1],
                    bias=gbias[:, 8 * b + m : 8 * b + m + 1],
                )
            for bb in range(2 if grp in S_MULT else 0):
                m, b = 4 * g + j, 2 * h + bb
                if G_MULT:
                    nc.gpsimd.tensor_scalar(
                        out=gam[grp][:, j, T * bb : T * bb + T],
                        in0=gam[grp][:, j, T * bb : T * bb + T],
                        scalar1=alpha[:, 8 * b + m : 8 * b + m + 1],
                        scalar2=0.0,
                        op0=ALU.mult,
                        op1=ALU.add,
                    )
                else:
                    nc.scalar.activation(
                        out=gam[grp][:, j, T * bb : T * bb + T],
                        in_=gam[grp][:, j, T * bb : T * bb + T],
                        func=AF.Copy,
                        scale=alpha[:, 8 * b + m : 8 * b + m + 1],
                    )

        wnat, wgt = {}, {}

        def weight_tile(s):
            return ((1, 2, 0)[s % 3], s // 3) if s < 12 else (3, s - 12)

        def w_load(s):
            wi, t4 = weight_tile(s)
            if wi < 3:
                view = weights[wi].rearrange("(g r u e) c -> r g u e c", r=P, u=2, e=2)[:, t4 // 2, t4 % 2, :, :]
            else:
                view = weights[wi].rearrange("(t e r) c -> r t e c", r=P, e=2)[:, t4, :, :]
            wn = wpool.tile([P, 2, C], BF16, tag="wnat", bufs=3, name="wnat")
            nc.sync.dma_start(out=wn[:, :, :], in_=view)
            wnat[s] = wn

        def w_transposes(s, g):
            bank = bank_tile("ps_w")
            for uu in range(2):
                for blk in range(2):
                    col = (2 * uu + blk) * P
                    nc.tensor.transpose(
                        bank[:, col : col + P],
                        wnat[s][:, blk, :].bitcast(F32)[:, 256 * g + uu : 256 * g + 256 : 2],
                        identF[:],
                    )
            return bank

        def w_evac(s, g, bank):
            if g == 0:
                wgt[s] = wpool.tile([P, 2, HALF], F32, tag="wg", bufs=2, align_bytes=64, name="wg")
            nc.scalar.copy(
                out=wgt[s][:, g, :].rearrange("p (o u) -> p o u", u=2),
                in_=bank[:].rearrange("p (u o) -> p o u", u=2),
            )

        def w_quant(s):
            wi, t4 = weight_tile(s)
            if wi == 3:
                for g in range(2):
                    nc.vector.quantize_mx(
                        out=woc[:, g, T * t4 : T * t4 + T].bitcast(FP8X4),
                        scales=wos[:, g, T * t4 : T * t4 + T],
                        in_=wgt[s][:, g, :].bitcast(BF16),
                    )
            else:
                nc.vector.quantize_mx(
                    out=wc[wi][:, t4, :, :].rearrange("p g o -> p (g o)").bitcast(FP8X4),
                    scales=ws[wi][:, t4, :, :].rearrange("p g o -> p (g o)"),
                    in_=wgt[s][:].rearrange("p g w -> p (g w)").bitcast(BF16),
                )

        planes = {}

        def regroup(grp, mix, engine):
            grouped = mid.tile([P, HALF, 4], BF16, tag="grouped", bufs=5, align_bytes=64, name="grouped")
            dst = grouped[:].rearrange("p (c i) j -> p c j i", i=4)
            src = planes[grp][mix][:].rearrange("p j (c i) -> p c j i", i=4)
            if engine == 0:
                nc.gpsimd.tensor_scalar(
                    out=grouped[:],
                    in0=planes[grp][mix][:].rearrange("p j t -> p t j"),
                    scalar1=1.0,
                    scalar2=0.0,
                    op0=ALU.mult,
                    op1=ALU.add,
                )
            elif engine == 1:
                nc.scalar.copy(out=dst, in_=src)
            else:
                nc.vector.tensor_copy(out=dst, in_=src)
            return (grp, mix, grouped)

        g_grouped = {}

        def g_regroup(grp, mix, half, gate_one):
            if half == 0:
                g_grouped[(grp, mix)] = mid.tile([P, HALF, 4], BF16, tag="grouped", bufs=5, align_bytes=64, name="grouped")
            tok = slice(T * half, T * half + T)
            nc.gpsimd.tensor_scalar(
                out=g_grouped[(grp, mix)][:, tok, :],
                in0=planes[grp][mix][:, :, tok].rearrange("p j t -> p t j"),
                scalar1=gate_one[:],
                scalar2=0.0,
                op0=ALU.mult,
                op1=ALU.add,
            )

        def quantise_mix(item):
            grp, mix, grouped = item
            h, g = grp // 2, grp % 2
            tok = slice(HALF * h, HALF * h + HALF)
            nc.vector.quantize_mx(
                out=xc[mix][:, g, tok].bitcast(FP8X4),
                scales=xsc[mix][:, g, tok],
                in_=grouped[:].rearrange("p t j -> p (t j)"),
            )

        def mixes_and_weights(pa):
            sm = pa.tile([P, 512], BF16, bufs=1, name="sm")
            sm2 = pa.tile([P, 512], BF16, bufs=1, name="sm2")
            nc.vector.memset(sm[:], 0.0)
            nc.vector.memset(epsT[:], EPS)
            nc.vector.memset(sm2[:], 0.0)
            make_identity(nc, identF[:])
            make_identity(nc, identB[:])
            nc.vector.tensor_scalar_mul(out=negB[:], in0=identB[:], scalar1=-1.0)
            nc.gpsimd.iota(
                iota1[:], pattern=[[1, T]], base=1, channel_multiplier=0, allow_small_or_imprecise_dtypes=True
            )
            diffB = pa.tile([P, P], BF16, bufs=1, name="diffB")
            nc.vector.tensor_copy(out=diffB[:, 0:1], in_=identB[:, 0:1])
            nc.vector.tensor_tensor(out=diffB[:, 1:P], in0=identB[:, 1:P], in1=identB[:, 0 : P - 1], op=ALU.subtract)
            smt = pa.tile([P, 36, 2], F32, bufs=1, name="smt")
            x_nat, dbank, t_grouped = {}, {}, {}
            diag = pa.tile([P, 2, 3, 4, P], BF16, bufs=1, name="diag")
            xw = pa.tile([P, 4, 4, T + 1], F32, bufs=1, name="xw")

            def load_x(h, cs):
                if h not in x_nat:
                    x_nat[h] = pa.tile([P, 4, C], BF16, tag="xnat", bufs=2, name="x_nat")
                rows = x_flat[HALF * h : HALF * h + HALF, cs]
                nc.sync.dma_start(out=x_nat[h][:, :, cs], in_=rows.rearrange("(i p) c -> p i c", p=P))

            def x_words(h, gu):
                bank = bank_tile("ps_x")
                for i in range(4):
                    nc.tensor.transpose(
                        bank[:, P * i : P * i + P],
                        x_nat[h][:, i, :].bitcast(F32)[:, 256 * (gu // 2) + gu % 2 : 256 * (gu // 2) + 256 : 2],
                        identF[:],
                    )
                dst = xw[:, gu, 2 * h : 2 * h + 2, 1 : T + 1]
                src = bank[:].rearrange("p (b t) -> p b t", t=T)
                if (h, gu) in X_VECTOR:
                    nc.vector.tensor_copy(out=dst, in_=src)
                else:
                    nc.scalar.copy(out=dst, in_=src)

            def t_mix(mix, i):
                h, g = TENSOR_GRP // 2, TENSOR_GRP % 2
                bank = bank_tile("ps_t")
                b, t0 = 2 * h + i // 2, P * (i % 2)
                for j in range(4):
                    words = xw[:, 2 * g + j // 2, b, :].bitcast(BF16).rearrange("p (t e) -> p t e", e=2)[:, :, j % 2]
                    now, before = words[:, t0 + 1 : t0 + 1 + P], words[:, t0 : t0 + P]
                    dst = bank[:, P * j : P * j + P]
                    nc.tensor.matmul(dst, lhsT=diag[:, 0, mix, j, :], rhs=now, start=True, stop=False)
                    nc.tensor.matmul(dst, lhsT=diag[:, 1, mix, j, :], rhs=before, start=False, stop=False)
                    nc.tensor.matmul(dst, lhsT=identB[:], rhs=before, start=False, stop=True)
                return bank

            def t_evac(mix, i, bank):
                if i == 0:
                    t_grouped[mix] = mid.tile([P, HALF, 4], BF16, tag="grouped", bufs=5, align_bytes=64, name="t_grouped")
                nc.scalar.copy(
                    out=t_grouped[mix][:, P * i : P * i + P, :], in_=bank[:].rearrange("p (j t) -> p t j", j=4)
                )

            def difference_plane(s):
                h, m = s // 8, s % 8
                bank = bank_tile("ps_d")
                lo, hi = 512 * (m // 4) + m % 4, 512 * (m // 4) + 512
                for i in range(4):
                    nc.tensor.matmul(
                        bank[:, P * i : P * i + P], lhsT=x_nat[h][:, i, lo:hi:4], rhs=diffB[:],
                        start=True, stop=False,
                    )
                    if i % 2 == 0:
                        before = sm[:, m % 4 : 512 : 4]
                        row = 2 * V_XP + 2 * (2 * h + i // 2) + m // 4
                    else:
                        before = x_nat[h][:, i - 1, lo:hi:4]
                        row = P - 1
                    nc.tensor.matmul(
                        bank[:, P * i : P * i + 1], lhsT=before, rhs=negB[:, row : row + 1], start=False, stop=True
                    )
                dbank[s] = bank

            def mix_plane(s):
                h, m = s // 8, s % 8
                gu, e, j, grp = m // 2, m % 2, m % 4, s // 4
                if j == 0:
                    planes[grp] = [
                        mid.tile([P, 4, HALF], BF16, tag="planes", bufs=5, name="planes%d" % i) for i in range(3)
                    ]
                shifted = xw[:, gu, 2 * h : 2 * h + 2, 0:T].bitcast(BF16).rearrange("p b (t e) -> p b t e", e=2)[:, :, :, e]
                for mix in range(3):
                    nc.vector.scalar_tensor_tensor(
                        out=planes[grp][mix][:, j, :].rearrange("p (b t) -> p b t", t=T),
                        in0=dbank[s][:].rearrange("p (b t) -> p b t", t=T),
                        scalar=scal(V_MUR + mix, m),
                        in1=shifted,
                        op0=ALU.mult,
                        op1=ALU.add,
                    )

            def ln_table(n):
                m, b = n // 4, n % 4
                nc.scalar.activation(
                    out=q[:, m, T * b : T * b + T], in_=dec[:, m, :], func=AF.Ln,
                    scale=scal(V_B0 + b, m), bias=epsT[:],
                )

            for v, vec in ((V_MUR, mu_r), (V_MUK, mu_k), (V_MUV, mu_v), (V_W, w), (V_U, u)):
                nc.scalar.dma_start(out=sm[2 * v : 2 * v + 2, :], in_=vec.rearrange("(r c) -> r c", c=512))
            warm = keep.tile([P, 1], F32)
            nc.scalar.activation(out=warm[:], in_=epsT[:], func=AF.Exp)
            load_x(0, slice(0, 512))
            nc.sync.dma_start(out=sm[2 * V_XP : 2 * V_XP + 8, :], in_=x_prev0.rearrange("b (r c) -> (b r) c", c=512))
            load_x(0, slice(512, C))
            nc.sync.dma_start(out=sm2[8:16, :], in_=b0.rearrange("b (r c) -> (b r) c", c=512))
            nc.sync.dma_start(out=sm2[0:8, :], in_=a0.rearrange("b (r c) -> (b r) c", c=512))
            for s in range(3):
                w_load(s)
            load_x(1, slice(0, C))

            def vector_words(tile, first, rows):
                bank = bank_tile("ps_sm")
                for uu in range(2):
                    nc.tensor.transpose(bank[:, P * uu : P * uu + P], tile[:].bitcast(F32)[:, uu:256:2], identF[:])
                words = smt[:, first : first + rows, :]
                nc.vector.tensor_copy(
                    out=words, in_=bank[:, 0:256].rearrange("p (u r) -> p r u", u=2)[:, 0:rows, :]
                )
                nc.vector.tensor_copy(
                    out=sc[:, 4 * first : 4 * first + 4 * rows], in_=words.rearrange("p r u -> p (r u)").bitcast(BF16)
                )

            if SM_FIRST:
                vector_words(sm, 0, 20)
                x_words(0, 0)
            else:
                x_words(0, 0)
                vector_words(sm, 0, 20)
            nc.vector.tensor_copy(
                out=xw[:, :, :, 0].rearrange("p (g u) b -> p g u b", u=2),
                in_=smt[:, 2 * V_XP : 2 * V_XP + 8, :].rearrange("p (b g) u -> p g u b", g=2),
            )
            nc.vector.tensor_scalar_mul(out=negw[:], in0=sc[:, 8 * V_W : 8 * V_W + 8], scalar1=-1.0)
            difference_plane(VECTOR_UNITS[0])
            difference_plane(VECTOR_UNITS[1])
            mix_plane(VECTOR_UNITS[0])
            vector_words(sm2, 20, 16)
            dec = gpool.tile([P, 8, T], F32, tag="gam", name="dec")
            for m in range(8):
                nc.scalar.activation(out=dec[:, m, :], in_=iota1[:], func=AF.Exp, scale=negw[:, m : m + 1])
            x_words(0, 1)
            for mix in range(3):
                for j in range(4):
                    mu = scal(V_MUR + mix, 4 * (TENSOR_GRP % 2) + j)
                    for sign, eye in ((0, identB), (1, negB)):
                        nc.gpsimd.tensor_scalar(
                            out=diag[:, sign, mix, j, :], in0=eye[:], scalar1=mu, scalar2=0.0, op0=ALU.mult, op1=ALU.add
                        )

            to_quantise = {n: [] for n in range(14)}
            w_quants = {n: [] for n in range(15)}
            t_next = w_done = 0
            for n in range(12):
                if n + 2 < 12:
                    difference_plane(VECTOR_UNITS[n + 2])
                for h, gu in X_STEPS.get(n, ()):
                    x_words(h, gu)
                w_banks = []
                for i in range(W_STEPS[n]):
                    w_banks.append((w_done, [w_transposes(w_done, g) for g in range(2)]))
                    w_load(w_done + 3)
                    w_done += 1
                if n == 4:
                    nc.vector.tensor_scalar_mul(out=negu[:], in0=sc[:, 8 * V_U : 8 * V_U + 8], scalar1=-1.0)
                if n == 5:
                    nc.vector.reciprocal(out=rb[:], in_=sc[:, 8 * V_B0 : 8 * V_B0 + 32])
                if n == 7:
                    nc.vector.tensor_tensor(
                        out=alpha[:], in0=sc[:, 8 * V_A0 : 8 * V_A0 + 32], in1=rb[:], op=ALU.mult
                    )
                if n == 6:
                    nc.vector.tensor_scalar_add(out=gbias[:], in0=gbias[:], scalar1=-math.log(EPS))
                t_banks = []
                for i in range(T_STEPS[n]):
                    t_banks.append((t_next, t_mix(t_next // 4, t_next % 4)))
                    t_next += 1
                for tile, banks in w_banks:
                    for g in range(2):
                        w_evac(tile, g, banks[g])
                    w_quants[n + W_LAG].append(tile)
                for t, bank in t_banks:
                    t_evac(t // 4, t % 4, bank)
                    if t % 4 == 3:
                        to_quantise[n + 1].append((TENSOR_GRP, t // 4, t_grouped[t // 4]))
                if n == 1:
                    nc.scalar.activation(out=gbias[:], in_=sc[:, 8 * V_B0 : 8 * V_B0 + 32], func=AF.Ln)
                for row in range(LN_ROWS[n], LN_ROWS[n + 1]):
                    ln_table(row)
                for grp, mix, half in G_RG.get(n, ()):
                    g_regroup(grp, mix, half, gate_one)
                    if half == 1:
                        to_quantise[n + 1].append((grp, mix, g_grouped[(grp, mix)]))
                for grp, mix in S_REGROUPS.get(n, ()):
                    to_quantise[n + 2].append(regroup(grp, mix, 1))
                for j in TABLE0.get(n, ()):
                    sigmoid_table(0, j)
                if n > 0:
                    mix_plane(VECTOR_UNITS[n])
                for tile in w_quants[n]:
                    w_quant(tile)
                for item in to_quantise[n]:
                    quantise_mix(item)
                for grp, mix in V_REGROUPS.get(n, ()):
                    to_quantise[n + 1].append(regroup(grp, mix, 2))
                if n + 1 in G_RG:
                    gate_one = pa.tile([P, 1], F32, tag="gate", bufs=2, name="gate_one")
                    nc.vector.memset(gate_one[:], 1.0)
            return [lambda tile=tile: w_quant(tile) for tile in w_quants[12] + w_quants[13]] + [lambda item=item: quantise_mix(item) for item in to_quantise[12] + to_quantise[13]]

        def stages(pb, late):
            acc, ygrp, wgrp, rgrp, ots, held = {}, {}, {}, {}, {}, {}

            def flat(t):
                return t[:].rearrange("p j t -> p (j t)")

            def runs_of_four(t, cols):
                return t[:, :, cols].rearrange("p j (c i) -> p c j i", i=4)

            def stage1_matmuls(un):
                h, m = un // 8, un % 8
                tok = slice(HALF * h, HALF * h + HALF)
                mc = slice(P * (m % 2), P * (m % 2) + P)
                for wi in (1, 2, 0):
                    ps = bank_tile("ps_s1")
                    for g in range(2):
                        nc.tensor.matmul_mx(
                            out=ps[:],
                            lhsT=wc[wi][:, m // 2, g, mc].bitcast(FP8X4),
                            lhsT_scale=ws[wi][:, m // 2, g, mc],
                            rhs=xc[wi][:, g, tok].bitcast(FP8X4),
                            rhs_scale=xsc[wi][:, g, tok],
                            start=(g == 0),
                            stop=(g == 1),
                        )
                    acc[(un, wi)] = ps

            def a_minus(grp, j, bb, operand):
                h, g = grp // 2, grp % 2
                cols = slice(T * bb, T * bb + T)
                m, b = 4 * g + j, 2 * h + bb
                nc.vector.scalar_tensor_tensor(
                    out=wgrp[grp][:, j, cols],
                    in0=gam[grp][:, j, cols],
                    scalar=alpha[:, 8 * b + m : 8 * b + m + 1],
                    in1=operand,
                    op0=ALU.mult,
                    op1=ALU.subtract,
                )

            def sigmoids(un):
                h, m = un // 8, un % 8
                j, grp = un % 4, un // 4
                tok = slice(HALF * h, HALF * h + HALF)
                if j == 0:
                    ygrp[grp] = pb.tile([P, 4, HALF], F32, tag="grp", bufs=6, name="ygrp")
                    wgrp[grp] = pb.tile([P, 4, HALF], F32, tag="grp", bufs=6, name="wgrp")
                    rgrp[grp] = pb.tile([P, 4, HALF], F32, tag="grp", bufs=6, name="rgrp")
                y_t = ygrp[grp][:, j, :]
                nc.vector.tensor_tensor(out=y_t, in0=acc[(un, 1)][:], in1=q[:, m, tok], op=ALU.subtract)
                if grp in PQ:
                    nc.scalar.activation(out=wgrp[grp][:, j, :], in_=y_t, func=AF.Sigmoid, bias=scal(V_U, m))
                    nc.scalar.activation(out=y_t, in_=y_t, func=AF.Sigmoid, scale=-1.0, bias=negu[:, m : m + 1])
                    if un < V_Q:
                        part = slice(0, G_COLS)
                        nc.gpsimd.tensor_tensor(
                            out=y_t[:, part], in0=gam[grp][:, j, part], in1=y_t[:, part], op=ALU.mult
                        )
                else:
                    nc.scalar.activation(out=y_t, in_=y_t, func=AF.Sigmoid, bias=scal(V_U, m))
                nc.scalar.activation(out=rgrp[grp][:, j, :], in_=acc[(un, 0)][:], func=AF.Sigmoid)

            def subtract_v(un):
                j, grp = un % 4, un // 4
                if grp in PQ:
                    nc.vector.tensor_tensor(
                        out=wgrp[grp][:, j, :], in0=acc[(un, 2)][:], in1=wgrp[grp][:, j, :], op=ALU.mult
                    )
                    return
                if grp in S_MULT:
                    nc.vector.tensor_tensor(
                        out=wgrp[grp][:, j, :], in0=gam[grp][:, j, :], in1=acc[(un, 2)][:], op=ALU.subtract
                    )
                else:
                    for bb in range(2):
                        a_minus(grp, j, bb, acc[(un, 2)][:, T * bb : T * bb + T])

            def gate(grp, lo, hi):
                cols = slice(lo, hi)
                grouped = mid.tile([P, hi - lo, 4], BF16, tag="grouped", bufs=5, align_bytes=64, name="grouped")
                nc.vector.tensor_tensor(
                    out=grouped[:].rearrange("p (c i) j -> p c j i", i=4),
                    in0=runs_of_four(wgrp[grp], cols),
                    in1=runs_of_four(rgrp[grp], cols),
                    op=ALU.mult,
                )
                return grouped

            def quantise_h(grp, lo, hi, grouped):
                h, g = grp // 2, grp % 2
                tok = slice(HALF * h + lo, HALF * h + hi)
                nc.vector.quantize_mx(
                    out=hc[:, g, tok].bitcast(FP8X4),
                    scales=hs[:, g, tok],
                    in_=grouped[:].rearrange("p t j -> p (t j)"),
                )

            def add_parts(grp, lo, hi):
                if grp in S_MULT:
                    part = wgrp[grp][:, :, lo:hi]
                    nc.vector.tensor_tensor(out=part, in0=part, in1=ygrp[grp][:, :, lo:hi], op=ALU.add)
                else:
                    h, g = grp // 2, grp % 2
                    for bb in range(lo // T, hi // T):
                        cols = slice(T * bb, T * bb + T)
                        for j in range(4):
                            m, b = 4 * g + j, 2 * h + bb
                            nc.vector.scalar_tensor_tensor(
                                out=wgrp[grp][:, j, cols],
                                in0=ygrp[grp][:, j, cols],
                                scalar=alpha[:, 8 * b + m : 8 * b + m + 1],
                                in1=wgrp[grp][:, j, cols],
                                op0=ALU.mult,
                                op1=ALU.add,
                            )

            def group_step(grp, k):
                h, g = grp // 2, grp % 2
                if grp in PQ and k < 2:
                    if k == 0 and G_COLS < HALF:
                        rest = ygrp[grp][:, :, G_COLS:HALF]
                        nc.vector.tensor_tensor(out=rest, in0=gam[grp][:, :, G_COLS:HALF], in1=rest, op=ALU.mult)
                    if k == 1:
                        add_parts(grp, 0, HALF)
                    return
                if k == 0:
                    nc.vector.tensor_tensor(out=flat(wgrp[grp]), in0=flat(wgrp[grp]), in1=flat(ygrp[grp]), op=ALU.mult)
                elif k == 1:
                    if grp in S_MULT:
                        nc.vector.tensor_tensor(
                            out=flat(wgrp[grp]), in0=flat(gam[grp]), in1=flat(wgrp[grp]), op=ALU.subtract
                        )
                    else:
                        for j in range(4):
                            for bb in range(2):
                                a_minus(grp, j, bb, wgrp[grp][:, j, T * bb : T * bb + T])
                elif k == 2:
                    held[grp] = gate(grp, 0, HALF)
                else:
                    quantise_h(grp, 0, HALF, held[grp])

            def stage2_pass(h, n, g, ps):
                tt, oh = n // 2, n % 2
                t0 = HALF * h + P * tt
                nc.tensor.matmul_mx(
                    out=ps[:],
                    lhsT=hc[:, g, t0 : t0 + P].bitcast(FP8X4),
                    lhsT_scale=hs[:, g, t0 : t0 + P],
                    rhs=woc[:, g, HALF * oh : HALF * oh + HALF].bitcast(FP8X4),
                    rhs_scale=wos[:, g, HALF * oh : HALF * oh + HALF],
                    start=(g == 0),
                    stop=(g == 1),
                )

            def stage2_tile(h, n):
                ps = bank_tile("ps_s2")
                stage2_pass(h, n, 0, ps)
                stage2_pass(h, n, 1, ps)
                stage2_out(h, n, ps, True)

            def stage2_out(h, n, ps, on_scalar):
                tt, oh = n // 2, n % 2
                t0 = HALF * h + P * tt
                if oh == 0:
                    ots[h] = mid.tile([P, C], F32, tag="planes", bufs=5, name="ot")
                dst = ots[h][:, HALF * oh : HALF * oh + HALF]
                if on_scalar:
                    nc.scalar.copy(out=dst, in_=ps[:])
                else:
                    nc.vector.tensor_copy(out=dst, in_=ps[:])
                if n >= 4 and h == 1:
                    cols = slice(HALF * oh, HALF * oh + HALF)
                    nc.sync.dma_start(out=out_flat[t0 : t0 + P, cols], in_=ots[h][:, cols])
                elif oh == 1:
                    nc.sync.dma_start(out=out_flat[t0 : t0 + P, :], in_=ots[h][:])

            w_next = W_FIRST
            last_regroup = {}
            def do_regroup(mix, engine):
                last_regroup[mix] = regroup(2, mix, engine)

            v_mixes = [mix for mix in range(3) if mix not in S_LATE.values()]
            for mix in v_mixes:
                late.append(lambda mix=mix: do_regroup(mix, 2))
            for mix in v_mixes + list(S_LATE.values()):
                late.append(lambda mix=mix: quantise_mix(last_regroup[mix]))
            def next_place(un):
                if NEXT0 <= un < 15:
                    sigmoid_table((un + 1) // 4, (un + 1) % 4)

            for un in range(4):
                stage1_matmuls(un)
                if un in S_LATE:
                    do_regroup(S_LATE[un], 1)
                if w_next < 12:
                    banks = [w_transposes(w_next, g) for g in range(2)]
                    if w_next + 3 < 16:
                        w_load(w_next + 3)
                else:
                    banks = []
                sigmoids(un)
                if 0 not in PQ:
                    subtract_v(un)
                elif un > 0:
                    subtract_v(un - 1)
                for g in range(len(banks)):
                    w_evac(w_next, g, banks[g])
                if w_next > W_FIRST:
                    w_quant(w_next - 1)
                if banks:
                    w_next += 1
                for i in range(LATE[un]):
                    if late:
                        late.pop(0)()
                next_place(un)
            open_banks = []
            for grp in range(4):
                for k in range(4):
                    if grp < 3:
                        un = 4 * grp + 4 + k
                        stage1_matmuls(un)
                        sigmoids(un)
                        if un // 4 in PQ:
                            if un > 4 * PQ[0]:
                                subtract_v(un - 1)
                            if PQ_LATE and grp in PQ:
                                if k >= 2:
                                    group_step(grp, k - 1)
                                if k == 0 and grp - 1 in PQ:
                                    group_step(grp - 1, 3)
                            else:
                                group_step(grp, k)
                        else:
                            if k > 0:
                                subtract_v(un)
                            group_step(grp, k)
                            if k == 0:
                                subtract_v(un)
                    while late and grp == 0:
                        late.pop(0)()
                    bs = 4 * grp + k
                    if bs == 0:
                        w_quant(11)
                    if bs in W_OUT:
                        tile = 12 + W_OUT.index(bs)
                        banks = [w_transposes(tile, g) for g in range(2)]
                        if tile == 12:
                            w_load(15)
                        for g in range(2):
                            w_evac(tile, g, banks[g])
                    if bs - 1 in W_OUT:
                        w_quant(12 + W_OUT.index(bs - 1))
                    if grp < 3:
                        next_place(4 * grp + 4 + k)
                    if grp == 2 and k >= 4 - S2_EARLY:
                        stage2_tile(0, k - 4 + S2_EARLY)
                    if grp == 3 and k == 0:
                        if PQ_LATE:
                            group_step(2, 3)
                        for n in range(S2_EARLY, 8):
                            stage2_tile(0, n)
                        for n in range(8):
                            open_banks.append(bank_tile("ps_s2"))
                            stage2_pass(1, n, 0, open_banks[n])
            def finish(tiles, on_vector):
                for n in tiles:
                    stage2_pass(1, n, 1, open_banks[n])
                    stage2_out(1, n, open_banks[n], n not in on_vector)

            half_t, last_t = T, T + P
            subtract_v(15)
            if G_COLS < HALF:
                rest = ygrp[3][:, 0 : V_Q - 12, G_COLS:HALF]
                nc.vector.tensor_tensor(out=rest, in0=gam[3][:, 0 : V_Q - 12, G_COLS:HALF], in1=rest, op=ALU.mult)
            for un in range(V_Q, 16):
                y_t = ygrp[3][:, un - 12, :]
                nc.vector.tensor_tensor(out=y_t, in0=gam[3][:, un - 12, :], in1=y_t, op=ALU.mult)
            add_parts(3, 0, half_t)
            add_parts(3, half_t, HALF)
            first = gate(3, 0, half_t)
            quantise_h(3, 0, half_t, first)
            finish((0, 1, 2), ())
            second = gate(3, half_t, last_t)
            third = gate(3, last_t, HALF)
            quantise_h(3, half_t, last_t, second)
            quantise_h(3, last_t, HALF, third)
            finish((3, 4, 5, 6, 7), (3, 5, 7))

        with tc.manual_schedule():
            with tc.tile_pool(name="pa", bufs=2) as pool_a:
                late = mixes_and_weights(pool_a)
            with tc.tile_pool(name="pb", bufs=2) as pool_b:
                stages(pool_b, late)
